import numpy as np
import ml_dtypes


def mxq(x, axis, fmt="e4m3"):
    dtype, down = {"e4m3": (ml_dtypes.float8_e4m3fn, 7), "e5m2": (ml_dtypes.float8_e5m2, 14)}[fmt]
    v = np.moveaxis(np.asarray(x, np.float32).astype(ml_dtypes.bfloat16).astype(np.float64), axis, -1)
    blocks = v.reshape(v.shape[:-1] + (-1, 32))
    amax = np.abs(blocks).max(-1, keepdims=True)
    byte = np.maximum(np.where(amax > 0, np.frexp(amax)[1] - 1 + 127, 0) - down, 1)
    scale = np.exp2(byte - 127.0)
    codes = (blocks / scale).astype(np.float32).astype(dtype).astype(np.float64)
    return np.moveaxis((codes * scale).reshape(v.shape), -1, axis)


WIDE = False


def mx_kscale(k):
    if not WIDE:
        return np.ones(k)
    levels = np.array([10, -10, 5, -5, 0])
    a = np.random.permutation(np.resize(levels, k // 512 * 4)).reshape(k // 512, 4)
    idx = np.arange(k)
    return np.exp2(a[idx // 512, idx % 128 // 32])


BF16 = ml_dtypes.bfloat16


def bf(x):
    return np.asarray(x, np.float32).astype(BF16)


def f64(x):
    return np.asarray(x).astype(np.float64)


B, C, HID, H, W = 2, 512, 64, 64, 64
N_P, N_H, N_F, N_U, N_L = 7, 3, 2, 4, 2
EPS = 1e-5


def setup_inputs():
    s = mx_kscale(C)
    off = 0.5 * np.random.standard_normal((1, C, 1, 1))
    return {
        "p_nodes": bf(np.random.standard_normal((N_P, B, HID, H, W))),
        "h_nodes": bf(np.random.standard_normal((N_H, B, HID, H, W))),
        "f_nodes": bf(np.random.standard_normal((N_F, B, HID, H, W))),
        "xp": bf((np.random.standard_normal((B, C, H, W)) + off) * s[None, :, None, None]),
        "h_att": bf(np.random.uniform(0.0, 1.0, (N_H, B, 1, H, W))),
        "Wu": bf(np.random.standard_normal((N_U * HID, C)) / np.sqrt(C) / s[None, :]),
        "Wl": bf(np.random.standard_normal((N_L * HID, C)) / np.sqrt(C) / s[None, :]),
        "gamma_u": bf(1.0 + 0.1 * np.random.standard_normal(N_U * HID)),
        "beta_u": bf(0.1 * np.random.standard_normal(N_U * HID)),
        "gamma_l": bf(1.0 + 0.1 * np.random.standard_normal(N_L * HID)),
        "beta_l": bf(0.1 * np.random.standard_normal(N_L * HID)),
    }


def conv_bn_relu(x, Wc, gamma, beta):
    y = (mxq(Wc, 1, "e4m3") @ mxq(x, 1, "e4m3").reshape(B, C, H * W)).reshape(B, -1, H, W)
    m = y.mean(axis=(0, 2, 3), keepdims=True)
    v = y.var(axis=(0, 2, 3), keepdims=True)
    y = (y - m) / np.sqrt(v + EPS)
    y = y * gamma[None, :, None, None] + beta[None, :, None, None]
    return np.maximum(y, 0.0)


def reference(p_nodes, h_nodes, f_nodes, xp, h_att, Wu, Wl, gamma_u, beta_u, gamma_l, beta_l):
    p_nodes, h_nodes, xp, h_att = f64(p_nodes), f64(h_nodes), f64(xp), f64(h_att)
    du = conv_bn_relu(h_att[1] * xp, f64(Wu), f64(gamma_u), f64(beta_u))
    dl = conv_bn_relu(h_att[2] * xp, f64(Wl), f64(gamma_l), f64(beta_l))
    du4 = du.reshape(B, N_U, HID, H, W).transpose(1, 0, 2, 3, 4)
    dl2 = dl.reshape(B, N_L, HID, H, W).transpose(1, 0, 2, 3, 4)
    p0 = 0.5 * (h_nodes[0] + p_nodes[0])
    p_up = 0.5 * (p_nodes[1:1 + N_U] + du4)
    p_low = 0.5 * (p_nodes[1 + N_U:N_P] + dl2)
    return np.concatenate([p0[None], p_up, p_low], axis=0)

@@ -1,0 +1,302 @@
+from contextlib import ExitStack
+
+import concourse.mybir as mybir
+from concourse.masks import make_identity
+
+F32 = mybir.dt.float32
+BF16 = mybir.dt.bfloat16
+U32 = mybir.dt.uint32
+U8 = mybir.dt.uint8
+FP8X4 = mybir.dt.float8_e4m3fn_x4
+ALU = mybir.AluOpType
+ACT = mybir.ActivationFunctionType
+AX = mybir.AxisListType
+
+P = 128
+PACK = 4
+BATCH = 2
+HID = 64
+PIX = 4096
+CH = 512
+CH_PER_IMAGE = PIX // CH
+N_CH = BATCH * CH_PER_IMAGE
+N_PIX = BATCH * PIX
+N_TILES = 3
+BRANCH = (0, 0, 1)
+EPS = 1e-5
+RAW_BUFS = 4
+GROUP = 4
+QUARTER = PIX // 4
+
+FLOPS = 2 * N_TILES * P * PACK * P * N_PIX
+BYTES = 2 * (7 * N_PIX * HID + N_PIX * HID + N_PIX * PACK * P + 2 * N_PIX + N_TILES * P * (PACK * P + 2)) + 4 * 7 * N_PIX * HID
+
+
+def tile_gnn_t_kernel(
+    tc, p_nodes, h_nodes, f_nodes, xp, h_att, Wu, Wl, gamma_u, beta_u, gamma_l, beta_l, out
+):
+    nc = tc.nc
+    with ExitStack() as ctx:
+        ctx.enter_context(tc.manual_schedule())
+        const = ctx.enter_context(tc.tile_pool(name="const", bufs=1))
+        keep = ctx.enter_context(tc.tile_pool(name="keep", bufs=1))
+
+        xp_rows = xp.rearrange("b (p j) h w -> b p j (h w)", j=PACK)
+        att_src = h_att[1:3].rearrange("i b o (hh hl) w -> (i b o hh) (hl w)", hl=2)
+
+        att_rows = const.tile([P, P], BF16)
+        nc.sync.dma_start(out=att_rows[:], in_=att_src)
+        w_rows = const.tile([P, N_TILES, PACK * P], BF16)
+        nc.sync.dma_start(out=w_rows[:, 0:2, :], in_=Wu.rearrange("(m q) c -> q m c", q=P))
+        nc.sync.dma_start(out=w_rows[:, 2, :], in_=Wl)
+        par_rows = const.tile([P, P], BF16)
+        nc.vector.memset(par_rows[:], 0.0)
+        nc.sync.dma_start(out=par_rows[0:2, :], in_=gamma_u.rearrange("(m q) -> m q", q=P))
+        nc.sync.dma_start(out=par_rows[2:3, :], in_=gamma_l.rearrange("(m q) -> m q", q=P))
+        nc.sync.dma_start(out=par_rows[3:5, :], in_=beta_u.rearrange("(m q) -> m q", q=P))
+        nc.sync.dma_start(out=par_rows[5:6, :], in_=beta_l.rearrange("(m q) -> m q", q=P))
+
+        ident_bf = const.tile([P, P], BF16)
+        make_identity(nc, ident_bf[:])
+        ident_f32 = const.tile([P, P], F32)
+        make_identity(nc, ident_f32[:])
+
+        one = const.tile([P, 1], F32)
+        nc.vector.memset(one[:], 1.0)
+        warm = const.tile([P, 1], F32)
+        nc.scalar.activation(out=warm[:], in_=one[:], func=ACT.Sqrt)
+
+        w_codes = keep.tile([P, N_TILES, P], U32, align_bytes=64)
+        w_scales = keep.tile([P, N_TILES, P], U8, align_bytes=64)
+        x_codes = keep.tile([P, N_CH, 2, CH], U32, align_bytes=64)
+        x_scales = keep.tile([P, N_CH, 2, CH], U8, align_bytes=64)
+        node_sb = keep.tile([P, N_TILES, BATCH, PIX], BF16)
+        par = keep.tile([P, 2 * N_TILES], F32)
+        half_gain = keep.tile([P, N_TILES], F32)
+        half_bias = keep.tile([P, N_TILES], F32)
+
+        def conv_pass(dst, m, c, start, stop):
+            nc.tensor.matmul_mx(
+                out=dst,
+                lhsT=w_codes[:, m, :].bitcast(FP8X4),
+                lhsT_scale=w_scales[:, m, :],
+                rhs=x_codes[:, c, BRANCH[m], :].bitcast(FP8X4),
+                rhs_scale=x_scales[:, c, BRANCH[m], :],
+                start=start,
+                stop=stop,
+            )
+
+        with ExitStack() as first:
+            raw_pool = first.enter_context(tc.tile_pool(name="raw", bufs=RAW_BUFS))
+            xg_pool = first.enter_context(tc.tile_pool(name="xg", bufs=3))
+            prod_pool = first.enter_context(tc.tile_pool(name="prod", bufs=4))
+            junk_pool = first.enter_context(tc.tile_pool(name="junk", bufs=4))
+            zero_pool = first.enter_context(tc.tile_pool(name="zero", bufs=1))
+            o0_pool = first.enter_context(tc.tile_pool(name="o0", bufs=2))
+            small = first.enter_context(tc.tile_pool(name="small", bufs=1))
+            psum_acc = first.enter_context(tc.psum_pool(name="psum_acc", bufs=1))
+            psum_att = first.enter_context(tc.psum_pool(name="psum_att", bufs=3))
+            psum_y = first.enter_context(tc.psum_pool(name="psum_y", bufs=2))
+
+            def load_chunk(c):
+                b, k = divmod(c, CH_PER_IMAGE)
+                raw = raw_pool.tile([P, PACK, CH], BF16, name="raw")
+                nc.sync.dma_start(out=raw[:], in_=xp_rows[b, :, :, k * CH : (k + 1) * CH])
+                return raw
+
+            raws = []
+            for c in range(RAW_BUFS):
+                raws.append(load_chunk(c))
+            p0 = zero_pool.tile([P, PIX], BF16)
+            nc.sync.dma_start(out=p0[:], in_=p_nodes[0].rearrange("b c h w -> (b c) (h w)"))
+            h0 = zero_pool.tile([P, PIX], BF16)
+            nc.sync.dma_start(out=h0[:], in_=h_nodes[0].rearrange("b c h w -> (b c) (h w)"))
+
+            att_t = psum_y.tile([P, P], BF16, tag="y")
+            nc.tensor.transpose(att_t[:], att_rows[:], ident_bf[:])
+            att_pairs = const.tile([P, P, 2], BF16)
+            nc.vector.tensor_copy(out=att_pairs[:], in_=att_t[:].unsqueeze(2).to_broadcast([P, P, 2]))
+            att_words = att_pairs[:].rearrange("q r e -> q (r e)").bitcast(F32)
+
+            w_grouped = const.tile([P, N_TILES, PACK * P], BF16, align_bytes=64)
+            for m in range(N_TILES):
+                w_words = w_rows[:, m, :].bitcast(F32)
+                w_t = psum_y.tile([P, 2, P], F32, tag="y")
+                for u in range(2):
+                    nc.tensor.transpose(w_t[:, u, :], w_words[:, u : 2 * P : 2], ident_f32[:])
+                nc.vector.tensor_copy(
+                    out=w_grouped[:, m, :].bitcast(F32).rearrange("p (h j u) -> p h j u", j=2, u=2),
+                    in_=w_t[:].rearrange("p u (j h) -> p h j u", j=2),
+                )
+            for m in range(N_TILES):
+                nc.vector.quantize_mx(
+                    out=w_codes[:, m, :].bitcast(FP8X4), scales=w_scales[:, m, :], in_=w_grouped[:, m, :]
+                )
+
+            par_mixed = const.tile([P, P], BF16)
+            nc.vector.tensor_copy(
+                out=par_mixed[:].rearrange("r (h j) -> r h j", j=2),
+                in_=par_rows[:].rearrange("r (j h) -> r h j", j=2),
+            )
+            par_t = psum_y.tile([P, P], BF16, tag="y")
+            nc.tensor.transpose(par_t[:], par_mixed[:], ident_bf[:])
+            nc.vector.tensor_copy(out=par[:], in_=par_t[:, 0 : 2 * N_TILES])
+
+            acc = []
+            for m in range(N_TILES):
+                acc.append(psum_acc.tile([P, CH], F32, name="acc%d" % m))
+            ssq = small.tile([P, N_TILES, N_CH], F32)
+
+            def regroup(raw):
+                xg = xg_pool.tile([P, CH, PACK], BF16, name="xg")
+                nc.scalar.copy(
+                    out=xg[:].rearrange("p (c i) t -> p c t i", i=4),
+                    in_=raw[:].rearrange("p t (c i) -> p c t i", i=4),
+                )
+                return xg
+
+            def spread_attention(c):
+                banks = []
+                for i in range(2):
+                    bank = psum_att.tile([P, CH], F32, name="att_bank")
+                    for s in range(CH // P):
+                        r = i * (N_PIX // P) + c * (CH // P) + s
+                        nc.tensor.transpose(
+                            bank[:, s * P : (s + 1) * P],
+                            att_words[:, r : r + 1].to_broadcast([P, P]),
+                            ident_f32[:],
+                        )
+                    banks.append(bank)
+                return banks
+
+            def weigh(xg, bank):
+                prod = prod_pool.tile([P, PACK * CH], BF16, name="prod", align_bytes=64)
+                nc.vector.tensor_tensor(
+                    out=prod[:].rearrange("p (w h e) -> p w h e", h=2, e=2),
+                    in0=xg[:].rearrange("p w (h e) -> p w h e", e=2),
+                    in1=bank[:]
+                    .bitcast(BF16)
+                    .rearrange("p (w e) -> p w e", e=2)
+                    .unsqueeze(2)
+                    .to_broadcast([P, CH, 2, 2]),
+                    op=ALU.mult,
+                )
+                return prod
+
+            def quantise(prod, c, i):
+                nc.vector.quantize_mx(
+                    out=x_codes[:, c, i, :].bitcast(FP8X4), scales=x_scales[:, c, i, :], in_=prod[:]
+                )
+
+            def node0_quarter(i):
+                cols = slice(i * QUARTER, (i + 1) * QUARTER)
+                nc.vector.tensor_scalar(
+                    out=h0[:, cols], in0=h0[:, cols], scalar1=0.5, scalar2=None, op0=ALU.mult
+                )
+                o0 = o0_pool.tile([P, QUARTER], F32, name="o0")
+                nc.vector.scalar_tensor_tensor(
+                    out=o0[:], in0=p0[:, cols], scalar=0.5, in1=h0[:, cols], op0=ALU.mult, op1=ALU.add
+                )
+                nc.sync.dma_start(out=out[0].rearrange("b c h w -> (b c) (h w)")[:, cols], in_=o0[:])
+
+            def load_node(k):
+                m, rest = divmod(k, 2 * BATCH)
+                b, j = divmod(rest, 2)
+                nc.sync.dma_start(
+                    out=node_sb[j:P:2, m, b, :],
+                    in_=p_nodes[1 + 2 * m + j, b].rearrange("c h w -> c (h w)"),
+                )
+
+            xgs = {}
+            banks = {}
+            prod_l = {}
+            for step in range(N_CH + 2):
+                if step < N_CH:
+                    xgs[step] = regroup(raws[step])
+                    if step + RAW_BUFS < N_CH:
+                        raws.append(load_chunk(step + RAW_BUFS))
+                    if step < N_TILES * BATCH * 2:
+                        load_node(step)
+                c = step - 1
+                if 0 <= c < N_CH:
+                    prod_u = weigh(xgs[c], banks[c][0])
+                    if c > 0:
+                        quantise(prod_l[c - 1], c - 1, 1)
+                    prod_l[c] = weigh(xgs[c], banks[c][1])
+                    quantise(prod_u, c, 0)
+                    if c % 4 == 3:
+                        node0_quarter(c // 4)
+                if c == N_CH:
+                    quantise(prod_l[c - 1], c - 1, 1)
+                if step < N_CH:
+                    banks[step] = spread_attention(step)
+                c = step - 2
+                if c >= 0:
+                    for m in range(N_TILES):
+                        y = psum_y.tile([P, CH], F32, tag="y")
+                        conv_pass(y[:], m, c, True, True)
+                        conv_pass(acc[m][:], m, c, c == 0, c == N_CH - 1)
+                        junk = junk_pool.tile([P, CH], BF16, name="junk")
+                        nc.scalar.activation(
+                            out=junk[:], in_=y[:], func=ACT.Square, accum_out=ssq[:, m, c : c + 1]
+                        )
+
+            sums = small.tile([P, N_TILES], F32)
+            for m in range(N_TILES):
+                nc.vector.tensor_reduce(out=sums[:, m : m + 1], in_=acc[m][:], axis=AX.X, op=ALU.add)
+            mean = small.tile([P, N_TILES], F32)
+            nc.vector.tensor_scalar(out=mean[:], in0=sums[:], scalar1=1.0 / N_PIX, scalar2=None, op0=ALU.mult)
+            mean_sq = small.tile([P, N_TILES], F32)
+            nc.vector.tensor_tensor(out=mean_sq[:], in0=mean[:], in1=mean[:], op=ALU.mult)
+            ssq_sum = small.tile([P, N_TILES], F32)
+            nc.vector.tensor_reduce(out=ssq_sum[:], in_=ssq[:], axis=AX.X, op=ALU.add)
+            var = small.tile([P, N_TILES], F32)
+            nc.vector.scalar_tensor_tensor(
+                out=var[:], in0=ssq_sum[:], scalar=1.0 / N_PIX, in1=mean_sq[:], op0=ALU.mult, op1=ALU.subtract
+            )
+            var_eps = small.tile([P, N_TILES], F32)
+            nc.vector.tensor_scalar(out=var_eps[:], in0=var[:], scalar1=0.0, scalar2=EPS, op0=ALU.max, op1=ALU.add)
+            std = small.tile([P, N_TILES], F32)
+            nc.scalar.activation(out=std[:], in_=var_eps[:], func=ACT.Sqrt)
+            rstd = small.tile([P, N_TILES], F32)
+            nc.vector.reciprocal(out=rstd[:], in_=std[:])
+            nc.vector.scalar_tensor_tensor(
+                out=half_gain[:], in0=rstd[:], scalar=0.5, in1=par[:, 0:N_TILES], op0=ALU.mult, op1=ALU.mult
+            )
+            shift = small.tile([P, N_TILES], F32)
+            nc.vector.tensor_tensor(out=shift[:], in0=mean[:], in1=half_gain[:], op=ALU.mult)
+            nc.vector.scalar_tensor_tensor(
+                out=half_bias[:],
+                in0=par[:, N_TILES : 2 * N_TILES],
+                scalar=0.5,
+                in1=shift[:],
+                op0=ALU.mult,
+                op1=ALU.subtract,
+            )
+
+        with ExitStack() as second:
+            t_pool = second.enter_context(tc.tile_pool(name="t", bufs=4))
+            psum_z = second.enter_context(tc.psum_pool(name="psum_z", bufs=8))
+            for m in range(N_TILES):
+                for g in range(N_CH // GROUP):
+                    b, part = divmod(g, CH_PER_IMAGE // GROUP)
+                    cols = slice(part * GROUP * CH, (part + 1) * GROUP * CH)
+                    t = t_pool.tile([P, GROUP * CH], F32, name="t")
+                    for k in range(GROUP):
+                        z = psum_z.tile([P, CH], F32, name="z")
+                        conv_pass(z[:], m, g * GROUP + k, True, True)
+                        nc.scalar.activation(
+                            out=t[:, k * CH : (k + 1) * CH],
+                            in_=z[:],
+                            func=ACT.Relu,
+                            scale=half_gain[:, m : m + 1],
+                            bias=half_bias[:, m : m + 1],
+                        )
+                    nc.vector.scalar_tensor_tensor(
+                        out=t[:], in0=node_sb[:, m, b, cols], scalar=0.5, in1=t[:], op0=ALU.mult, op1=ALU.add
+                    )
+                    for j in range(2):
+                        nc.sync.dma_start(
+                            out=out[1 + 2 * m + j, b].rearrange("c h w -> c (h w)")[:, cols],
+                            in_=t[j:P:2, :],
+                        )

@@ -25,7 +25,9 @@ N_TILES = 3
 BRANCH = (0, 0, 1)
 EPS = 1e-5
 RAW_BUFS = 4
-GROUP = 4
+GROUP = 2
+T_BUFS = 10
+V_PIX = 64
 QUARTER = PIX // 4
 
 FLOPS = 2 * N_TILES * P * PACK * P * N_PIX
@@ -45,16 +47,9 @@ def tile_gnn_t_kernel(
         att_src = h_att[1:3].rearrange("i b o (hh hl) w -> (i b o hh) (hl w)", hl=2)
 
         att_rows = const.tile([P, P], BF16)
-        nc.sync.dma_start(out=att_rows[:], in_=att_src)
         w_rows = const.tile([P, N_TILES, PACK * P], BF16)
-        nc.sync.dma_start(out=w_rows[:, 0:2, :], in_=Wu.rearrange("(m q) c -> q m c", q=P))
-        nc.sync.dma_start(out=w_rows[:, 2, :], in_=Wl)
         par_rows = const.tile([P, P], BF16)
         nc.vector.memset(par_rows[:], 0.0)
-        nc.sync.dma_start(out=par_rows[0:2, :], in_=gamma_u.rearrange("(m q) -> m q", q=P))
-        nc.sync.dma_start(out=par_rows[2:3, :], in_=gamma_l.rearrange("(m q) -> m q", q=P))
-        nc.sync.dma_start(out=par_rows[3:5, :], in_=beta_u.rearrange("(m q) -> m q", q=P))
-        nc.sync.dma_start(out=par_rows[5:6, :], in_=beta_l.rearrange("(m q) -> m q", q=P))
 
         ident_bf = const.tile([P, P], BF16)
         make_identity(nc, ident_bf[:])
@@ -104,9 +99,16 @@ def tile_gnn_t_kernel(
                 nc.sync.dma_start(out=raw[:], in_=xp_rows[b, :, :, k * CH : (k + 1) * CH])
                 return raw
 
-            raws = []
-            for c in range(RAW_BUFS):
+            raws = [load_chunk(0)]
+            nc.sync.dma_start(out=att_rows[:], in_=att_src)
+            nc.sync.dma_start(out=w_rows[:, 0:2, :], in_=Wu.rearrange("(m q) c -> q m c", q=P))
+            nc.sync.dma_start(out=w_rows[:, 2, :], in_=Wl)
+            for c in range(1, RAW_BUFS):
                 raws.append(load_chunk(c))
+            nc.sync.dma_start(out=par_rows[0:2, :], in_=gamma_u.rearrange("(m q) -> m q", q=P))
+            nc.sync.dma_start(out=par_rows[2:3, :], in_=gamma_l.rearrange("(m q) -> m q", q=P))
+            nc.sync.dma_start(out=par_rows[3:5, :], in_=beta_u.rearrange("(m q) -> m q", q=P))
+            nc.sync.dma_start(out=par_rows[5:6, :], in_=beta_l.rearrange("(m q) -> m q", q=P))
             p0 = zero_pool.tile([P, PIX], BF16)
             nc.sync.dma_start(out=p0[:], in_=p_nodes[0].rearrange("b c h w -> (b c) (h w)"))
             h0 = zero_pool.tile([P, PIX], BF16)
@@ -133,15 +135,6 @@ def tile_gnn_t_kernel(
                     out=w_codes[:, m, :].bitcast(FP8X4), scales=w_scales[:, m, :], in_=w_grouped[:, m, :]
                 )
 
-            par_mixed = const.tile([P, P], BF16)
-            nc.vector.tensor_copy(
-                out=par_mixed[:].rearrange("r (h j) -> r h j", j=2),
-                in_=par_rows[:].rearrange("r (j h) -> r h j", j=2),
-            )
-            par_t = psum_y.tile([P, P], BF16, tag="y")
-            nc.tensor.transpose(par_t[:], par_mixed[:], ident_bf[:])
-            nc.vector.tensor_copy(out=par[:], in_=par_t[:, 0 : 2 * N_TILES])
-
             acc = []
             for m in range(N_TILES):
                 acc.append(psum_acc.tile([P, CH], F32, name="acc%d" % m))
@@ -149,9 +142,13 @@ def tile_gnn_t_kernel(
 
             def regroup(raw):
                 xg = xg_pool.tile([P, CH, PACK], BF16, name="xg")
+                nc.vector.tensor_copy(
+                    out=xg[:, 0:V_PIX, :].rearrange("p (c i) t -> p c t i", i=4),
+                    in_=raw[:, :, 0:V_PIX].rearrange("p t (c i) -> p c t i", i=4),
+                )
                 nc.scalar.copy(
-                    out=xg[:].rearrange("p (c i) t -> p c t i", i=4),
-                    in_=raw[:].rearrange("p t (c i) -> p c t i", i=4),
+                    out=xg[:, V_PIX:CH, :].rearrange("p (c i) t -> p c t i", i=4),
+                    in_=raw[:, :, V_PIX:CH].rearrange("p t (c i) -> p c t i", i=4),
                 )
                 return xg
 
@@ -241,6 +238,15 @@ def tile_gnn_t_kernel(
                             out=junk[:], in_=y[:], func=ACT.Square, accum_out=ssq[:, m, c : c + 1]
                         )
 
+            par_mixed = const.tile([P, P], BF16)
+            nc.vector.tensor_copy(
+                out=par_mixed[:].rearrange("r (h j) -> r h j", j=2),
+                in_=par_rows[:].rearrange("r (j h) -> r h j", j=2),
+            )
+            par_t = psum_y.tile([P, P], BF16, tag="y")
+            nc.tensor.transpose(par_t[:], par_mixed[:], ident_bf[:])
+            nc.vector.tensor_copy(out=par[:], in_=par_t[:, 0 : 2 * N_TILES])
+
             sums = small.tile([P, N_TILES], F32)
             for m in range(N_TILES):
                 nc.vector.tensor_reduce(out=sums[:, m : m + 1], in_=acc[m][:], axis=AX.X, op=ALU.add)
@@ -275,7 +281,7 @@ def tile_gnn_t_kernel(
             )
 
         with ExitStack() as second:
-            t_pool = second.enter_context(tc.tile_pool(name="t", bufs=4))
+            t_pool = second.enter_context(tc.tile_pool(name="t", bufs=T_BUFS))
             psum_z = second.enter_context(tc.psum_pool(name="psum_z", bufs=8))
             for m in range(N_TILES):
                 for g in range(N_CH // GROUP):

@@ -27,8 +27,7 @@ EPS = 1e-5
 RAW_BUFS = 4
 GROUP = 2
 T_BUFS = 10
-V_PIX = 64
-QUARTER = PIX // 4
+V_PIX = 128
 
 FLOPS = 2 * N_TILES * P * PACK * P * N_PIX
 BYTES = 2 * (7 * N_PIX * HID + N_PIX * HID + N_PIX * PACK * P + 2 * N_PIX + N_TILES * P * (PACK * P + 2)) + 4 * 7 * N_PIX * HID
@@ -87,7 +86,7 @@ def tile_gnn_t_kernel(
             prod_pool = first.enter_context(tc.tile_pool(name="prod", bufs=4))
             junk_pool = first.enter_context(tc.tile_pool(name="junk", bufs=4))
             zero_pool = first.enter_context(tc.tile_pool(name="zero", bufs=1))
-            o0_pool = first.enter_context(tc.tile_pool(name="o0", bufs=2))
+            o0_pool = first.enter_context(tc.tile_pool(name="o0", bufs=3))
             small = first.enter_context(tc.tile_pool(name="small", bufs=1))
             psum_acc = first.enter_context(tc.psum_pool(name="psum_acc", bufs=1))
             psum_att = first.enter_context(tc.psum_pool(name="psum_att", bufs=3))
@@ -152,19 +151,16 @@ def tile_gnn_t_kernel(
                 )
                 return xg
 
-            def spread_attention(c):
-                banks = []
-                for i in range(2):
-                    bank = psum_att.tile([P, CH], F32, name="att_bank")
-                    for s in range(CH // P):
-                        r = i * (N_PIX // P) + c * (CH // P) + s
-                        nc.tensor.transpose(
-                            bank[:, s * P : (s + 1) * P],
-                            att_words[:, r : r + 1].to_broadcast([P, P]),
-                            ident_f32[:],
-                        )
-                    banks.append(bank)
-                return banks
+            def spread_attention(c, i):
+                bank = psum_att.tile([P, CH], F32, name="att_bank")
+                for s in range(CH // P):
+                    r = i * (N_PIX // P) + c * (CH // P) + s
+                    nc.tensor.transpose(
+                        bank[:, s * P : (s + 1) * P],
+                        att_words[:, r : r + 1].to_broadcast([P, P]),
+                        ident_f32[:],
+                    )
+                return bank
 
             def weigh(xg, bank):
                 prod = prod_pool.tile([P, PACK * CH], BF16, name="prod", align_bytes=64)
@@ -185,16 +181,21 @@ def tile_gnn_t_kernel(
                     out=x_codes[:, c, i, :].bitcast(FP8X4), scales=x_scales[:, c, i, :], in_=prod[:]
                 )
 
-            def node0_quarter(i):
-                cols = slice(i * QUARTER, (i + 1) * QUARTER)
-                nc.vector.tensor_scalar(
-                    out=h0[:, cols], in0=h0[:, cols], scalar1=0.5, scalar2=None, op0=ALU.mult
-                )
-                o0 = o0_pool.tile([P, QUARTER], F32, name="o0")
-                nc.vector.scalar_tensor_tensor(
-                    out=o0[:], in0=p0[:, cols], scalar=0.5, in1=h0[:, cols], op0=ALU.mult, op1=ALU.add
-                )
+            def node0_bank(i):
+                cols = slice(i * CH, (i + 1) * CH)
+                both = psum_y.tile([P, CH], F32, tag="y")
+                nc.tensor.matmul(out=both[:], lhsT=ident_bf[:], rhs=p0[:, cols], start=True, stop=False)
+                nc.tensor.matmul(out=both[:], lhsT=ident_bf[:], rhs=h0[:, cols], start=False, stop=True)
+                o0 = o0_pool.tile([P, CH], F32, name="o0")
+                nc.scalar.mul(out=o0[:], in_=both[:], mul=0.5)
                 nc.sync.dma_start(out=out[0].rearrange("b c h w -> (b c) (h w)")[:, cols], in_=o0[:])
+
+            def conv_and_square(m, c):
+                y = psum_y.tile([P, CH], F32, tag="y")
+                conv_pass(y[:], m, c, True, True)
+                conv_pass(acc[m][:], m, c, c == 0, c == N_CH - 1)
+                junk = junk_pool.tile([P, CH], BF16, name="junk")
+                nc.scalar.activation(out=junk[:], in_=y[:], func=ACT.Square, accum_out=ssq[:, m, c : c + 1])
 
             def load_node(k):
                 m, rest = divmod(k, 2 * BATCH)
@@ -216,27 +217,25 @@ def tile_gnn_t_kernel(
                         load_node(step)
                 c = step - 1
                 if 0 <= c < N_CH:
-                    prod_u = weigh(xgs[c], banks[c][0])
+                    prod_u = weigh(xgs[c], banks[c, 0])
                     if c > 0:
                         quantise(prod_l[c - 1], c - 1, 1)
-                    prod_l[c] = weigh(xgs[c], banks[c][1])
+                    prod_l[c] = weigh(xgs[c], banks[c, 1])
                     quantise(prod_u, c, 0)
-                    if c % 4 == 3:
-                        node0_quarter(c // 4)
                 if c == N_CH:
                     quantise(prod_l[c - 1], c - 1, 1)
-                if step < N_CH:
-                    banks[step] = spread_attention(step)
                 c = step - 2
+                if step < N_CH:
+                    banks[step, 0] = spread_attention(step, 0)
                 if c >= 0:
-                    for m in range(N_TILES):
-                        y = psum_y.tile([P, CH], F32, tag="y")
-                        conv_pass(y[:], m, c, True, True)
-                        conv_pass(acc[m][:], m, c, c == 0, c == N_CH - 1)
-                        junk = junk_pool.tile([P, CH], BF16, name="junk")
-                        nc.scalar.activation(
-                            out=junk[:], in_=y[:], func=ACT.Square, accum_out=ssq[:, m, c : c + 1]
-                        )
+                    conv_and_square(0, c)
+                    conv_and_square(1, c)
+                if step < N_CH:
+                    banks[step, 1] = spread_attention(step, 1)
+                if c >= 0:
+                    conv_and_square(2, c)
+                    if c % 2 == 1:
+                        node0_bank(c // 2)
 
             par_mixed = const.tile([P, P], BF16)
             nc.vector.tensor_copy(
@@ -245,15 +244,19 @@ def tile_gnn_t_kernel(
             )
             par_t = psum_y.tile([P, P], BF16, tag="y")
             nc.tensor.transpose(par_t[:], par_mixed[:], ident_bf[:])
-            nc.vector.tensor_copy(out=par[:], in_=par_t[:, 0 : 2 * N_TILES])
+            nc.vector.tensor_scalar(
+                out=par[:], in0=par_t[:, 0 : 2 * N_TILES], scalar1=0.5, scalar2=None, op0=ALU.mult
+            )
 
             sums = small.tile([P, N_TILES], F32)
             for m in range(N_TILES):
                 nc.vector.tensor_reduce(out=sums[:, m : m + 1], in_=acc[m][:], axis=AX.X, op=ALU.add)
-            mean = small.tile([P, N_TILES], F32)
-            nc.vector.tensor_scalar(out=mean[:], in0=sums[:], scalar1=1.0 / N_PIX, scalar2=None, op0=ALU.mult)
+            neg_mean = small.tile([P, N_TILES], F32)
+            nc.vector.tensor_scalar(
+                out=neg_mean[:], in0=sums[:], scalar1=-1.0 / N_PIX, scalar2=None, op0=ALU.mult
+            )
             mean_sq = small.tile([P, N_TILES], F32)
-            nc.vector.tensor_tensor(out=mean_sq[:], in0=mean[:], in1=mean[:], op=ALU.mult)
+            nc.vector.tensor_tensor(out=mean_sq[:], in0=neg_mean[:], in1=neg_mean[:], op=ALU.mult)
             ssq_sum = small.tile([P, N_TILES], F32)
             nc.vector.tensor_reduce(out=ssq_sum[:], in_=ssq[:], axis=AX.X, op=ALU.add)
             var = small.tile([P, N_TILES], F32)
@@ -266,19 +269,16 @@ def tile_gnn_t_kernel(
             nc.scalar.activation(out=std[:], in_=var_eps[:], func=ACT.Sqrt)
             rstd = small.tile([P, N_TILES], F32)
             nc.vector.reciprocal(out=rstd[:], in_=std[:])
-            nc.vector.scalar_tensor_tensor(
-                out=half_gain[:], in0=rstd[:], scalar=0.5, in1=par[:, 0:N_TILES], op0=ALU.mult, op1=ALU.mult
-            )
-            shift = small.tile([P, N_TILES], F32)
-            nc.vector.tensor_tensor(out=shift[:], in0=mean[:], in1=half_gain[:], op=ALU.mult)
-            nc.vector.scalar_tensor_tensor(
-                out=half_bias[:],
-                in0=par[:, N_TILES : 2 * N_TILES],
-                scalar=0.5,
-                in1=shift[:],
-                op0=ALU.mult,
-                op1=ALU.subtract,
-            )
+            nc.vector.tensor_tensor(out=half_gain[:], in0=rstd[:], in1=par[:, 0:N_TILES], op=ALU.mult)
+            for m in range(N_TILES):
+                nc.vector.scalar_tensor_tensor(
+                    out=half_bias[:, m : m + 1],
+                    in0=neg_mean[:, m : m + 1],
+                    scalar=half_gain[:, m : m + 1],
+                    in1=par[:, N_TILES + m : N_TILES + m + 1],
+                    op0=ALU.mult,
+                    op1=ALU.add,
+                )
 
         with ExitStack() as second:
             t_pool = second.enter_context(tc.tile_pool(name="t", bufs=T_BUFS))

@@ -27,7 +27,9 @@ EPS = 1e-5
 RAW_BUFS = 4
 GROUP = 2
 T_BUFS = 10
-V_PIX = 128
+G_PIX = 224
+S_PIX = CH - G_PIX
+SLOTS = 4
 
 FLOPS = 2 * N_TILES * P * PACK * P * N_PIX
 BYTES = 2 * (7 * N_PIX * HID + N_PIX * HID + N_PIX * PACK * P + 2 * N_PIX + N_TILES * P * (PACK * P + 2)) + 4 * 7 * N_PIX * HID
@@ -82,8 +84,7 @@ def tile_gnn_t_kernel(
 
         with ExitStack() as first:
             raw_pool = first.enter_context(tc.tile_pool(name="raw", bufs=RAW_BUFS))
-            xg_pool = first.enter_context(tc.tile_pool(name="xg", bufs=3))
-            prod_pool = first.enter_context(tc.tile_pool(name="prod", bufs=4))
+            work_pool = first.enter_context(tc.tile_pool(name="work", bufs=1))
             junk_pool = first.enter_context(tc.tile_pool(name="junk", bufs=4))
             zero_pool = first.enter_context(tc.tile_pool(name="zero", bufs=1))
             o0_pool = first.enter_context(tc.tile_pool(name="o0", bufs=3))
@@ -139,17 +140,25 @@ def tile_gnn_t_kernel(
                 acc.append(psum_acc.tile([P, CH], F32, name="acc%d" % m))
             ssq = small.tile([P, N_TILES, N_CH], F32)
 
-            def regroup(raw):
-                xg = xg_pool.tile([P, CH, PACK], BF16, name="xg")
-                nc.vector.tensor_copy(
-                    out=xg[:, 0:V_PIX, :].rearrange("p (c i) t -> p c t i", i=4),
-                    in_=raw[:, :, 0:V_PIX].rearrange("p t (c i) -> p c t i", i=4),
-                )
+            work = work_pool.tile([P, SLOTS, 2 * PACK * CH], BF16, align_bytes=64)
+
+            def grouped(s):
+                return work[:, (s + 1) % SLOTS, 0 : PACK * CH]
+
+            def regroup(raw, s):
+                xg = grouped(s).rearrange("p (w t) -> p w t", t=PACK)
                 nc.scalar.copy(
-                    out=xg[:, V_PIX:CH, :].rearrange("p (c i) t -> p c t i", i=4),
-                    in_=raw[:, :, V_PIX:CH].rearrange("p t (c i) -> p c t i", i=4),
+                    out=xg[:, 0:S_PIX, :].rearrange("p (c i) t -> p c t i", i=4),
+                    in_=raw[:, :, 0:S_PIX].rearrange("p t (c i) -> p c t i", i=4),
                 )
-                return xg
+                nc.gpsimd.tensor_scalar(
+                    out=xg[:, S_PIX:CH, :],
+                    in0=raw[:, :, S_PIX:CH].rearrange("p t w -> p w t"),
+                    scalar1=1.0,
+                    scalar2=0.0,
+                    op0=ALU.mult,
+                    op1=ALU.add,
+                )
 
             def spread_attention(c, i):
                 bank = psum_att.tile([P, CH], F32, name="att_bank")
@@ -162,11 +171,12 @@ def tile_gnn_t_kernel(
                     )
                 return bank
 
-            def weigh(xg, bank):
-                prod = prod_pool.tile([P, PACK * CH], BF16, name="prod", align_bytes=64)
+            def weigh(c, i, bank):
                 nc.vector.tensor_tensor(
-                    out=prod[:].rearrange("p (w h e) -> p w h e", h=2, e=2),
-                    in0=xg[:].rearrange("p w (h e) -> p w h e", e=2),
+                    out=work[:, c % SLOTS, i * PACK * CH : (i + 1) * PACK * CH].rearrange(
+                        "p (w h e) -> p w h e", h=2, e=2
+                    ),
+                    in0=grouped(c).rearrange("p (w h e) -> p w h e", h=2, e=2),
                     in1=bank[:]
                     .bitcast(BF16)
                     .rearrange("p (w e) -> p w e", e=2)
@@ -174,11 +184,12 @@ def tile_gnn_t_kernel(
                     .to_broadcast([P, CH, 2, 2]),
                     op=ALU.mult,
                 )
-                return prod
 
-            def quantise(prod, c, i):
+            def quantise(c):
                 nc.vector.quantize_mx(
-                    out=x_codes[:, c, i, :].bitcast(FP8X4), scales=x_scales[:, c, i, :], in_=prod[:]
+                    out=x_codes[:, c, :, :].rearrange("p i w -> p (i w)").bitcast(FP8X4),
+                    scales=x_scales[:, c, :, :].rearrange("p i w -> p (i w)"),
+                    in_=work[:, c % SLOTS, :],
                 )
 
             def node0_bank(i):
@@ -205,26 +216,22 @@ def tile_gnn_t_kernel(
                     in_=p_nodes[1 + 2 * m + j, b].rearrange("c h w -> c (h w)"),
                 )
 
-            xgs = {}
             banks = {}
-            prod_l = {}
-            for step in range(N_CH + 2):
+            for step in range(N_CH + 3):
                 if step < N_CH:
-                    xgs[step] = regroup(raws[step])
+                    regroup(raws[step], step)
                     if step + RAW_BUFS < N_CH:
                         raws.append(load_chunk(step + RAW_BUFS))
                     if step < N_TILES * BATCH * 2:
                         load_node(step)
                 c = step - 1
                 if 0 <= c < N_CH:
-                    prod_u = weigh(xgs[c], banks[c, 0])
-                    if c > 0:
-                        quantise(prod_l[c - 1], c - 1, 1)
-                    prod_l[c] = weigh(xgs[c], banks[c, 1])
-                    quantise(prod_u, c, 0)
-                if c == N_CH:
-                    quantise(prod_l[c - 1], c - 1, 1)
+                    weigh(c, 0, banks[c, 0])
+                    weigh(c, 1, banks[c, 1])
                 c = step - 2
+                if 0 <= c < N_CH:
+                    quantise(c)
+                c = step - 3
                 if step < N_CH:
                     banks[step, 0] = spread_attention(step, 0)
                 if c >= 0:

@@ -24,12 +24,22 @@ N_PIX = BATCH * PIX
 N_TILES = 3
 BRANCH = (0, 0, 1)
 EPS = 1e-5
-RAW_BUFS = 4
-GROUP = 2
-T_BUFS = 10
 G_PIX = 224
 S_PIX = CH - G_PIX
-SLOTS = 4
+SUM_W = 256
+
+CHUNK_EL = PACK * CH
+RAW_SLOTS = 4
+WORK_SLOTS = 4
+WORK_0 = RAW_SLOTS * CHUNK_EL
+ARENA_EL = WORK_0 + WORK_SLOTS * 2 * CHUNK_EL
+REGION_EL = 2 * CHUNK_EL
+N_REGIONS = ARENA_EL // REGION_EL
+
+SUM_BANKS = (0, 1, 2)
+ATT_BANKS = (3, 4, 5)
+Y_BANKS = (6, 7)
+Z_BANKS = (3, 4, 5, 6, 7, 0, 1, 2)
 
 FLOPS = 2 * N_TILES * P * PACK * P * N_PIX
 BYTES = 2 * (7 * N_PIX * HID + N_PIX * HID + N_PIX * PACK * P + 2 * N_PIX + N_TILES * P * (PACK * P + 2)) + 4 * 7 * N_PIX * HID
@@ -43,6 +53,17 @@ def tile_gnn_t_kernel(
         ctx.enter_context(tc.manual_schedule())
         const = ctx.enter_context(tc.tile_pool(name="const", bufs=1))
         keep = ctx.enter_context(tc.tile_pool(name="keep", bufs=1))
+        junk_pool = ctx.enter_context(tc.tile_pool(name="junk", bufs=4))
+        o0_pool = ctx.enter_context(tc.tile_pool(name="o0", bufs=3))
+        psum = ctx.enter_context(tc.psum_pool(name="psum", bufs=1))
+
+        taken = {"att": 0, "y": 0, "z": 0}
+
+        def next_bank(ring, key, shape, dtype):
+            k = ring[taken[key] % len(ring)]
+            taken[key] = taken[key] + 1
+            got = psum.tile(shape, dtype, tag="bank%d" % k, name="bank%d" % k)
+            return got
 
         xp_rows = xp.rearrange("b (p j) h w -> b p j (h w)", j=PACK)
         att_src = h_att[1:3].rearrange("i b o (hh hl) w -> (i b o hh) (hl w)", hl=2)
@@ -67,217 +88,217 @@ def tile_gnn_t_kernel(
         x_codes = keep.tile([P, N_CH, 2, CH], U32, align_bytes=64)
         x_scales = keep.tile([P, N_CH, 2, CH], U8, align_bytes=64)
         node_sb = keep.tile([P, N_TILES, BATCH, PIX], BF16)
-        par = keep.tile([P, 2 * N_TILES], F32)
-        half_gain = keep.tile([P, N_TILES], F32)
-        half_bias = keep.tile([P, N_TILES], F32)
+        arena = keep.tile([P, ARENA_EL], BF16, align_bytes=64)
+        p0 = keep.tile([P, PIX], BF16)
+        h0 = keep.tile([P, PIX], BF16)
 
-        def conv_pass(dst, m, c, start, stop):
+        def conv_pass(dst, m, c, lo, hi, start, stop):
             nc.tensor.matmul_mx(
                 out=dst,
                 lhsT=w_codes[:, m, :].bitcast(FP8X4),
                 lhsT_scale=w_scales[:, m, :],
-                rhs=x_codes[:, c, BRANCH[m], :].bitcast(FP8X4),
-                rhs_scale=x_scales[:, c, BRANCH[m], :],
+                rhs=x_codes[:, c, BRANCH[m], lo:hi].bitcast(FP8X4),
+                rhs_scale=x_scales[:, c, BRANCH[m], lo:hi],
                 start=start,
                 stop=stop,
             )
 
-        with ExitStack() as first:
-            raw_pool = first.enter_context(tc.tile_pool(name="raw", bufs=RAW_BUFS))
-            work_pool = first.enter_context(tc.tile_pool(name="work", bufs=1))
-            junk_pool = first.enter_context(tc.tile_pool(name="junk", bufs=4))
-            zero_pool = first.enter_context(tc.tile_pool(name="zero", bufs=1))
-            o0_pool = first.enter_context(tc.tile_pool(name="o0", bufs=3))
-            small = first.enter_context(tc.tile_pool(name="small", bufs=1))
-            psum_acc = first.enter_context(tc.psum_pool(name="psum_acc", bufs=1))
-            psum_att = first.enter_context(tc.psum_pool(name="psum_att", bufs=3))
-            psum_y = first.enter_context(tc.psum_pool(name="psum_y", bufs=2))
+        def raw_slot(s):
+            k = s % RAW_SLOTS
+            return arena[:, k * CHUNK_EL : (k + 1) * CHUNK_EL].rearrange("p (t w) -> p t w", t=PACK)
 
-            def load_chunk(c):
-                b, k = divmod(c, CH_PER_IMAGE)
-                raw = raw_pool.tile([P, PACK, CH], BF16, name="raw")
-                nc.sync.dma_start(out=raw[:], in_=xp_rows[b, :, :, k * CH : (k + 1) * CH])
-                return raw
+        def work_slot(c):
+            k = c % WORK_SLOTS
+            return arena[:, WORK_0 + k * 2 * CHUNK_EL : WORK_0 + (k + 1) * 2 * CHUNK_EL]
 
-            raws = [load_chunk(0)]
-            nc.sync.dma_start(out=att_rows[:], in_=att_src)
-            nc.sync.dma_start(out=w_rows[:, 0:2, :], in_=Wu.rearrange("(m q) c -> q m c", q=P))
-            nc.sync.dma_start(out=w_rows[:, 2, :], in_=Wl)
-            for c in range(1, RAW_BUFS):
-                raws.append(load_chunk(c))
-            nc.sync.dma_start(out=par_rows[0:2, :], in_=gamma_u.rearrange("(m q) -> m q", q=P))
-            nc.sync.dma_start(out=par_rows[2:3, :], in_=gamma_l.rearrange("(m q) -> m q", q=P))
-            nc.sync.dma_start(out=par_rows[3:5, :], in_=beta_u.rearrange("(m q) -> m q", q=P))
-            nc.sync.dma_start(out=par_rows[5:6, :], in_=beta_l.rearrange("(m q) -> m q", q=P))
-            p0 = zero_pool.tile([P, PIX], BF16)
-            nc.sync.dma_start(out=p0[:], in_=p_nodes[0].rearrange("b c h w -> (b c) (h w)"))
-            h0 = zero_pool.tile([P, PIX], BF16)
-            nc.sync.dma_start(out=h0[:], in_=h_nodes[0].rearrange("b c h w -> (b c) (h w)"))
+        def grouped(s):
+            return work_slot(s + 1)[:, 0:CHUNK_EL]
 
-            att_t = psum_y.tile([P, P], BF16, tag="y")
-            nc.tensor.transpose(att_t[:], att_rows[:], ident_bf[:])
-            att_pairs = const.tile([P, P, 2], BF16)
-            nc.vector.tensor_copy(out=att_pairs[:], in_=att_t[:].unsqueeze(2).to_broadcast([P, P, 2]))
-            att_words = att_pairs[:].rearrange("q r e -> q (r e)").bitcast(F32)
+        def load_chunk(c):
+            b, k = divmod(c, CH_PER_IMAGE)
+            nc.sync.dma_start(out=raw_slot(c), in_=xp_rows[b, :, :, k * CH : (k + 1) * CH])
 
-            w_grouped = const.tile([P, N_TILES, PACK * P], BF16, align_bytes=64)
+        nc.sync.dma_start(out=att_rows[:], in_=att_src)
+        load_chunk(0)
+        nc.sync.dma_start(out=w_rows[:, 0:2, :], in_=Wu.rearrange("(m q) c -> q m c", q=P))
+        nc.sync.dma_start(out=w_rows[:, 2, :], in_=Wl)
+        for c in range(1, RAW_SLOTS):
+            load_chunk(c)
+        nc.sync.dma_start(out=par_rows[0:2, :], in_=gamma_u.rearrange("(m q) -> m q", q=P))
+        nc.sync.dma_start(out=par_rows[2:3, :], in_=gamma_l.rearrange("(m q) -> m q", q=P))
+        nc.sync.dma_start(out=par_rows[3:5, :], in_=beta_u.rearrange("(m q) -> m q", q=P))
+        nc.sync.dma_start(out=par_rows[5:6, :], in_=beta_l.rearrange("(m q) -> m q", q=P))
+        nc.sync.dma_start(out=p0[:], in_=p_nodes[0].rearrange("b c h w -> (b c) (h w)"))
+        nc.sync.dma_start(out=h0[:], in_=h_nodes[0].rearrange("b c h w -> (b c) (h w)"))
+
+        att_t = next_bank(Y_BANKS, "y", [P, P], BF16)
+        nc.tensor.transpose(att_t[:], att_rows[:], ident_bf[:])
+        att_pairs = const.tile([P, P, 2], BF16)
+        nc.vector.tensor_copy(out=att_pairs[:], in_=att_t[:].unsqueeze(2).to_broadcast([P, P, 2]))
+        att_words = att_pairs[:].rearrange("q r e -> q (r e)").bitcast(F32)
+
+        w_grouped = const.tile([P, N_TILES, PACK * P], BF16, align_bytes=64)
+
+        def turn_weights():
             for m in range(N_TILES):
                 w_words = w_rows[:, m, :].bitcast(F32)
-                w_t = psum_y.tile([P, 2, P], F32, tag="y")
+                w_t = next_bank(Y_BANKS, "y", [P, 2, P], F32)
                 for u in range(2):
                     nc.tensor.transpose(w_t[:, u, :], w_words[:, u : 2 * P : 2], ident_f32[:])
-                nc.vector.tensor_copy(
+                nc.scalar.copy(
                     out=w_grouped[:, m, :].bitcast(F32).rearrange("p (h j u) -> p h j u", j=2, u=2),
                     in_=w_t[:].rearrange("p u (j h) -> p h j u", j=2),
                 )
+
+        def quantise_weights():
             for m in range(N_TILES):
                 nc.vector.quantize_mx(
                     out=w_codes[:, m, :].bitcast(FP8X4), scales=w_scales[:, m, :], in_=w_grouped[:, m, :]
                 )
 
-            acc = []
-            for m in range(N_TILES):
-                acc.append(psum_acc.tile([P, CH], F32, name="acc%d" % m))
-            ssq = small.tile([P, N_TILES, N_CH], F32)
+        acc = []
+        for m in range(N_TILES):
+            acc_m = psum.tile([P, SUM_W], F32, tag="bank%d" % SUM_BANKS[m], name="acc%d" % m)
+            acc.append(acc_m)
+        ssq = keep.tile([P, N_TILES, N_CH], F32)
 
-            work = work_pool.tile([P, SLOTS, 2 * PACK * CH], BF16, align_bytes=64)
-
-            def grouped(s):
-                return work[:, (s + 1) % SLOTS, 0 : PACK * CH]
-
-            def regroup(raw, s):
-                xg = grouped(s).rearrange("p (w t) -> p w t", t=PACK)
-                nc.scalar.copy(
-                    out=xg[:, 0:S_PIX, :].rearrange("p (c i) t -> p c t i", i=4),
-                    in_=raw[:, :, 0:S_PIX].rearrange("p t (c i) -> p c t i", i=4),
-                )
-                nc.gpsimd.tensor_scalar(
-                    out=xg[:, S_PIX:CH, :],
-                    in0=raw[:, :, S_PIX:CH].rearrange("p t w -> p w t"),
-                    scalar1=1.0,
-                    scalar2=0.0,
-                    op0=ALU.mult,
-                    op1=ALU.add,
-                )
-
-            def spread_attention(c, i):
-                bank = psum_att.tile([P, CH], F32, name="att_bank")
-                for s in range(CH // P):
-                    r = i * (N_PIX // P) + c * (CH // P) + s
-                    nc.tensor.transpose(
-                        bank[:, s * P : (s + 1) * P],
-                        att_words[:, r : r + 1].to_broadcast([P, P]),
-                        ident_f32[:],
-                    )
-                return bank
-
-            def weigh(c, i, bank):
-                nc.vector.tensor_tensor(
-                    out=work[:, c % SLOTS, i * PACK * CH : (i + 1) * PACK * CH].rearrange(
-                        "p (w h e) -> p w h e", h=2, e=2
-                    ),
-                    in0=grouped(c).rearrange("p (w h e) -> p w h e", h=2, e=2),
-                    in1=bank[:]
-                    .bitcast(BF16)
-                    .rearrange("p (w e) -> p w e", e=2)
-                    .unsqueeze(2)
-                    .to_broadcast([P, CH, 2, 2]),
-                    op=ALU.mult,
-                )
-
-            def quantise(c):
-                nc.vector.quantize_mx(
-                    out=x_codes[:, c, :, :].rearrange("p i w -> p (i w)").bitcast(FP8X4),
-                    scales=x_scales[:, c, :, :].rearrange("p i w -> p (i w)"),
-                    in_=work[:, c % SLOTS, :],
-                )
-
-            def node0_bank(i):
-                cols = slice(i * CH, (i + 1) * CH)
-                both = psum_y.tile([P, CH], F32, tag="y")
-                nc.tensor.matmul(out=both[:], lhsT=ident_bf[:], rhs=p0[:, cols], start=True, stop=False)
-                nc.tensor.matmul(out=both[:], lhsT=ident_bf[:], rhs=h0[:, cols], start=False, stop=True)
-                o0 = o0_pool.tile([P, CH], F32, name="o0")
-                nc.scalar.mul(out=o0[:], in_=both[:], mul=0.5)
-                nc.sync.dma_start(out=out[0].rearrange("b c h w -> (b c) (h w)")[:, cols], in_=o0[:])
-
-            def conv_and_square(m, c):
-                y = psum_y.tile([P, CH], F32, tag="y")
-                conv_pass(y[:], m, c, True, True)
-                conv_pass(acc[m][:], m, c, c == 0, c == N_CH - 1)
-                junk = junk_pool.tile([P, CH], BF16, name="junk")
-                nc.scalar.activation(out=junk[:], in_=y[:], func=ACT.Square, accum_out=ssq[:, m, c : c + 1])
-
-            def load_node(k):
-                m, rest = divmod(k, 2 * BATCH)
-                b, j = divmod(rest, 2)
-                nc.sync.dma_start(
-                    out=node_sb[j:P:2, m, b, :],
-                    in_=p_nodes[1 + 2 * m + j, b].rearrange("c h w -> c (h w)"),
-                )
-
-            banks = {}
-            for step in range(N_CH + 3):
-                if step < N_CH:
-                    regroup(raws[step], step)
-                    if step + RAW_BUFS < N_CH:
-                        raws.append(load_chunk(step + RAW_BUFS))
-                    if step < N_TILES * BATCH * 2:
-                        load_node(step)
-                c = step - 1
-                if 0 <= c < N_CH:
-                    weigh(c, 0, banks[c, 0])
-                    weigh(c, 1, banks[c, 1])
-                c = step - 2
-                if 0 <= c < N_CH:
-                    quantise(c)
-                c = step - 3
-                if step < N_CH:
-                    banks[step, 0] = spread_attention(step, 0)
-                if c >= 0:
-                    conv_and_square(0, c)
-                    conv_and_square(1, c)
-                if step < N_CH:
-                    banks[step, 1] = spread_attention(step, 1)
-                if c >= 0:
-                    conv_and_square(2, c)
-                    if c % 2 == 1:
-                        node0_bank(c // 2)
-
-            par_mixed = const.tile([P, P], BF16)
-            nc.vector.tensor_copy(
-                out=par_mixed[:].rearrange("r (h j) -> r h j", j=2),
-                in_=par_rows[:].rearrange("r (j h) -> r h j", j=2),
+        def regroup(s):
+            raw = raw_slot(s)
+            xg = grouped(s).rearrange("p (w t) -> p w t", t=PACK)
+            s_end = S_PIX if s > 0 else CH // 4
+            g_start = S_PIX if s > 0 else 3 * CH // 4
+            nc.scalar.copy(
+                out=xg[:, 0:s_end, :].rearrange("p (c i) t -> p c t i", i=4),
+                in_=raw[:, :, 0:s_end].rearrange("p t (c i) -> p c t i", i=4),
             )
-            par_t = psum_y.tile([P, P], BF16, tag="y")
-            nc.tensor.transpose(par_t[:], par_mixed[:], ident_bf[:])
-            nc.vector.tensor_scalar(
-                out=par[:], in0=par_t[:, 0 : 2 * N_TILES], scalar1=0.5, scalar2=None, op0=ALU.mult
+            if g_start > s_end:
+                nc.vector.tensor_copy(
+                    out=xg[:, s_end:g_start, :].rearrange("p (c i) t -> p c t i", i=4),
+                    in_=raw[:, :, s_end:g_start].rearrange("p t (c i) -> p c t i", i=4),
+                )
+            nc.gpsimd.tensor_scalar(
+                out=xg[:, g_start:CH, :],
+                in0=raw[:, :, g_start:CH].rearrange("p t w -> p w t"),
+                scalar1=1.0,
+                scalar2=0.0,
+                op0=ALU.mult,
+                op1=ALU.add,
             )
 
-            sums = small.tile([P, N_TILES], F32)
-            for m in range(N_TILES):
+        def spread_attention(c, i):
+            bank = next_bank(ATT_BANKS, "att", [P, CH], F32)
+            for s in range(CH // P):
+                r = i * (N_PIX // P) + c * (CH // P) + s
+                nc.tensor.transpose(
+                    bank[:, s * P : (s + 1) * P],
+                    att_words[:, r : r + 1].to_broadcast([P, P]),
+                    ident_f32[:],
+                )
+            return bank
+
+        def weigh(c, i, bank):
+            nc.vector.tensor_tensor(
+                out=work_slot(c)[:, i * CHUNK_EL : (i + 1) * CHUNK_EL].rearrange(
+                    "p (w h e) -> p w h e", h=2, e=2
+                ),
+                in0=grouped(c).rearrange("p (w h e) -> p w h e", h=2, e=2),
+                in1=bank[:]
+                .bitcast(BF16)
+                .rearrange("p (w e) -> p w e", e=2)
+                .unsqueeze(2)
+                .to_broadcast([P, CH, 2, 2]),
+                op=ALU.mult,
+            )
+
+        def quantise(c):
+            nc.vector.quantize_mx(
+                out=x_codes[:, c, :, :].rearrange("p i w -> p (i w)").bitcast(FP8X4),
+                scales=x_scales[:, c, :, :].rearrange("p i w -> p (i w)"),
+                in_=work_slot(c),
+            )
+
+        def quantise_branch(c, i):
+            nc.vector.quantize_mx(
+                out=x_codes[:, c, i, :].bitcast(FP8X4),
+                scales=x_scales[:, c, i, :],
+                in_=work_slot(c)[:, i * CHUNK_EL : (i + 1) * CHUNK_EL],
+            )
+
+        def node0_bank(i):
+            cols = slice(i * CH, (i + 1) * CH)
+            both = next_bank(Y_BANKS, "y", [P, CH], F32)
+            nc.tensor.matmul(out=both[:], lhsT=ident_bf[:], rhs=p0[:, cols], start=True, stop=False)
+            nc.tensor.matmul(out=both[:], lhsT=ident_bf[:], rhs=h0[:, cols], start=False, stop=True)
+            o0 = o0_pool.tile([P, CH], F32, name="o0")
+            nc.scalar.mul(out=o0[:], in_=both[:], mul=0.5)
+            nc.sync.dma_start(out=out[0].rearrange("b c h w -> (b c) (h w)")[:, cols], in_=o0[:])
+
+        def conv_and_square(m, c):
+            y = next_bank(Y_BANKS, "y", [P, CH], F32)
+            conv_pass(y[:], m, c, 0, CH, True, True)
+            for q in range(CH // SUM_W):
+                conv_pass(
+                    acc[m][:],
+                    m,
+                    c,
+                    q * SUM_W,
+                    (q + 1) * SUM_W,
+                    c == 0 and q == 0,
+                    c == N_CH - 1 and q == CH // SUM_W - 1,
+                )
+            junk = junk_pool.tile([P, CH], BF16, name="junk")
+            nc.scalar.activation(out=junk[:], in_=y[:], func=ACT.Square, accum_out=ssq[:, m, c : c + 1])
+
+        def load_node(k):
+            m, rest = divmod(k, 2 * BATCH)
+            b, j = divmod(rest, 2)
+            nc.sync.dma_start(
+                out=node_sb[j:P:2, m, b, :],
+                in_=p_nodes[1 + 2 * m + j, b].rearrange("c h w -> c (h w)"),
+            )
+
+        par_mixed = const.tile([P, P], BF16)
+        par = keep.tile([P, 2 * N_TILES], F32)
+        sums = keep.tile([P, N_TILES], F32)
+        neg_mean = keep.tile([P, N_TILES], F32)
+        mean_sq = keep.tile([P, N_TILES], F32)
+        ssq_sum = keep.tile([P, N_TILES], F32)
+        var = keep.tile([P, N_TILES], F32)
+        var_eps = keep.tile([P, N_TILES], F32)
+        std = keep.tile([P, N_TILES], F32)
+        rstd = keep.tile([P, N_TILES], F32)
+        half_gain = keep.tile([P, N_TILES], F32)
+        half_bias = keep.tile([P, N_TILES], F32)
+
+        def variance(lo, hi):
+            for m in range(lo, hi):
                 nc.vector.tensor_reduce(out=sums[:, m : m + 1], in_=acc[m][:], axis=AX.X, op=ALU.add)
-            neg_mean = small.tile([P, N_TILES], F32)
             nc.vector.tensor_scalar(
-                out=neg_mean[:], in0=sums[:], scalar1=-1.0 / N_PIX, scalar2=None, op0=ALU.mult
+                out=neg_mean[:, lo:hi], in0=sums[:, lo:hi], scalar1=-1.0 / N_PIX, scalar2=None, op0=ALU.mult
             )
-            mean_sq = small.tile([P, N_TILES], F32)
-            nc.vector.tensor_tensor(out=mean_sq[:], in0=neg_mean[:], in1=neg_mean[:], op=ALU.mult)
-            ssq_sum = small.tile([P, N_TILES], F32)
-            nc.vector.tensor_reduce(out=ssq_sum[:], in_=ssq[:], axis=AX.X, op=ALU.add)
-            var = small.tile([P, N_TILES], F32)
+            nc.vector.tensor_tensor(
+                out=mean_sq[:, lo:hi], in0=neg_mean[:, lo:hi], in1=neg_mean[:, lo:hi], op=ALU.mult
+            )
+            nc.vector.tensor_reduce(out=ssq_sum[:, lo:hi], in_=ssq[:, lo:hi, :], axis=AX.X, op=ALU.add)
             nc.vector.scalar_tensor_tensor(
-                out=var[:], in0=ssq_sum[:], scalar=1.0 / N_PIX, in1=mean_sq[:], op0=ALU.mult, op1=ALU.subtract
+                out=var[:, lo:hi],
+                in0=ssq_sum[:, lo:hi],
+                scalar=1.0 / N_PIX,
+                in1=mean_sq[:, lo:hi],
+                op0=ALU.mult,
+                op1=ALU.subtract,
             )
-            var_eps = small.tile([P, N_TILES], F32)
-            nc.vector.tensor_scalar(out=var_eps[:], in0=var[:], scalar1=0.0, scalar2=EPS, op0=ALU.max, op1=ALU.add)
-            std = small.tile([P, N_TILES], F32)
-            nc.scalar.activation(out=std[:], in_=var_eps[:], func=ACT.Sqrt)
-            rstd = small.tile([P, N_TILES], F32)
-            nc.vector.reciprocal(out=rstd[:], in_=std[:])
-            nc.vector.tensor_tensor(out=half_gain[:], in0=rstd[:], in1=par[:, 0:N_TILES], op=ALU.mult)
-            for m in range(N_TILES):
+            nc.vector.tensor_scalar(
+                out=var_eps[:, lo:hi], in0=var[:, lo:hi], scalar1=0.0, scalar2=EPS, op0=ALU.max, op1=ALU.add
+            )
+
+        def root(lo, hi):
+            nc.scalar.activation(out=std[:, lo:hi], in_=var_eps[:, lo:hi], func=ACT.Sqrt)
+
+        def gain_and_bias(lo, hi):
+            nc.vector.reciprocal(out=rstd[:, lo:hi], in_=std[:, lo:hi])
+            nc.vector.tensor_tensor(out=half_gain[:, lo:hi], in0=rstd[:, lo:hi], in1=par[:, lo:hi], op=ALU.mult)
+            for m in range(lo, hi):
                 nc.vector.scalar_tensor_tensor(
                     out=half_bias[:, m : m + 1],
                     in0=neg_mean[:, m : m + 1],
@@ -287,29 +308,101 @@ def tile_gnn_t_kernel(
                     op1=ALU.add,
                 )
 
-        with ExitStack() as second:
-            t_pool = second.enter_context(tc.tile_pool(name="t", bufs=T_BUFS))
-            psum_z = second.enter_context(tc.psum_pool(name="psum_z", bufs=8))
-            for m in range(N_TILES):
-                for g in range(N_CH // GROUP):
-                    b, part = divmod(g, CH_PER_IMAGE // GROUP)
-                    cols = slice(part * GROUP * CH, (part + 1) * GROUP * CH)
-                    t = t_pool.tile([P, GROUP * CH], F32, name="t")
-                    for k in range(GROUP):
-                        z = psum_z.tile([P, CH], F32, name="z")
-                        conv_pass(z[:], m, g * GROUP + k, True, True)
-                        nc.scalar.activation(
-                            out=t[:, k * CH : (k + 1) * CH],
-                            in_=z[:],
-                            func=ACT.Relu,
-                            scale=half_gain[:, m : m + 1],
-                            bias=half_bias[:, m : m + 1],
-                        )
+        banks = {}
+        for step in range(N_CH + 3):
+            if step < N_CH:
+                regroup(step)
+                if step + RAW_SLOTS < N_CH:
+                    load_chunk(step + RAW_SLOTS)
+                if step < N_TILES * BATCH * 2:
+                    load_node(step)
+            c = step - 1
+            if c == N_CH - 1:
+                quantise(c - 1)
+            if 0 <= c < N_CH:
+                weigh(c, 0, banks[c, 0])
+                weigh(c, 1, banks[c, 1])
+            if c == N_CH - 1:
+                quantise_branch(c, 0)
+                quantise_branch(c, 1)
+            c = step - 2
+            if 0 <= c < N_CH - 2:
+                quantise(c)
+            if step == 1:
+                quantise_weights()
+                nc.vector.tensor_copy(
+                    out=par_mixed[:].rearrange("r (h j) -> r h j", j=2),
+                    in_=par_rows[:].rearrange("r (j h) -> r h j", j=2),
+                )
+            if step == 2:
+                par_t = next_bank(Y_BANKS, "y", [P, P], BF16)
+                nc.tensor.transpose(par_t[:], par_mixed[:], ident_bf[:])
+                nc.vector.tensor_scalar(
+                    out=par[:], in0=par_t[:, 0 : 2 * N_TILES], scalar1=0.5, scalar2=None, op0=ALU.mult
+                )
+            c = step - 3
+            last = c == N_CH - 1
+            if step < N_CH:
+                banks[step, 0] = spread_attention(step, 0)
+            if c >= 0:
+                conv_and_square(0, c)
+                conv_and_square(1, c)
+            if last:
+                variance(0, 1)
+                root(0, 1)
+            if step < N_CH:
+                banks[step, 1] = spread_attention(step, 1)
+            if step == 0:
+                turn_weights()
+            if c >= 0:
+                conv_and_square(2, c)
+            if last:
+                gain_and_bias(0, 1)
+                variance(1, N_TILES)
+            if step % 2 == 1 and 3 <= step <= 2 * CH_PER_IMAGE + 1:
+                node0_bank((step - 3) // 2)
+
+        groups = []
+        for m in range(N_TILES):
+            for b in range(BATCH):
+                sizes = (4, 4)
+                if (m, b) == (0, 0):
+                    sizes = (1, 1, 2, 4)
+                if (m, b) == (N_TILES - 1, BATCH - 1):
+                    sizes = (4, 2, 1, 1)
+                k0 = 0
+                for n in sizes:
+                    groups.append((m, b, k0, n))
+                    k0 += n
+        for g, (m, b, k0, n) in enumerate(groups):
+            r = g % N_REGIONS
+            t = arena[:, r * REGION_EL : r * REGION_EL + 2 * n * CH].bitcast(F32)
+            cols = slice(k0 * CH, (k0 + n) * CH)
+            for k in range(n):
+                z = next_bank(Z_BANKS, "z", [P, CH], F32)
+                conv_pass(z[:], m, b * CH_PER_IMAGE + k0 + k, 0, CH, True, True)
+                nc.scalar.activation(
+                    out=t[:, k * CH : (k + 1) * CH],
+                    in_=z[:],
+                    func=ACT.Relu,
+                    scale=half_gain[:, m : m + 1],
+                    bias=half_bias[:, m : m + 1],
+                )
+                if k % 2 == 1 or k == n - 1 or g >= len(groups) - 3:
+                    a = k - 1 if (k % 2 == 1 and g < len(groups) - 3) else k
                     nc.vector.scalar_tensor_tensor(
-                        out=t[:], in0=node_sb[:, m, b, cols], scalar=0.5, in1=t[:], op0=ALU.mult, op1=ALU.add
+                        out=t[:, a * CH : (k + 1) * CH],
+                        in0=node_sb[:, m, b, (k0 + a) * CH : (k0 + k + 1) * CH],
+                        scalar=0.5,
+                        in1=t[:, a * CH : (k + 1) * CH],
+                        op0=ALU.mult,
+                        op1=ALU.add,
                     )
-                    for j in range(2):
-                        nc.sync.dma_start(
-                            out=out[1 + 2 * m + j, b].rearrange("c h w -> c (h w)")[:, cols],
-                            in_=t[j:P:2, :],
-                        )
+            for j in range(2):
+                nc.sync.dma_start(
+                    out=out[1 + 2 * m + j, b].rearrange("c h w -> c (h w)")[:, cols],
+                    in_=t[j:P:2, :],
+                )
+            if g == 1:
+                root(1, N_TILES)
+                gain_and_bias(1, N_TILES)

@@ -37,8 +37,8 @@ REGION_EL = 2 * CHUNK_EL
 N_REGIONS = ARENA_EL // REGION_EL
 
 SUM_BANKS = (0, 1, 2)
-ATT_BANKS = (3, 4, 5)
-Y_BANKS = (6, 7)
+ATT_BANKS = (3, 4)
+Y_BANKS = (5, 6, 7)
 Z_BANKS = (3, 4, 5, 6, 7, 0, 1, 2)
 
 FLOPS = 2 * N_TILES * P * PACK * P * N_PIX
@@ -233,9 +233,12 @@ def tile_gnn_t_kernel(
             nc.scalar.mul(out=o0[:], in_=both[:], mul=0.5)
             nc.sync.dma_start(out=out[0].rearrange("b c h w -> (b c) (h w)")[:, cols], in_=o0[:])
 
-        def conv_and_square(m, c):
+        def conv(m, c):
             y = next_bank(Y_BANKS, "y", [P, CH], F32)
             conv_pass(y[:], m, c, 0, CH, True, True)
+            return y
+
+        def add_to_sum(m, c):
             for q in range(CH // SUM_W):
                 conv_pass(
                     acc[m][:],
@@ -246,6 +249,8 @@ def tile_gnn_t_kernel(
                     c == 0 and q == 0,
                     c == N_CH - 1 and q == CH // SUM_W - 1,
                 )
+
+        def square(y, m, c):
             junk = junk_pool.tile([P, CH], BF16, name="junk")
             nc.scalar.activation(out=junk[:], in_=y[:], func=ACT.Square, accum_out=ssq[:, m, c : c + 1])
 
@@ -341,26 +346,30 @@ def tile_gnn_t_kernel(
                     out=par[:], in0=par_t[:, 0 : 2 * N_TILES], scalar1=0.5, scalar2=None, op0=ALU.mult
                 )
             c = step - 3
-            last = c == N_CH - 1
-            if step < N_CH:
-                banks[step, 0] = spread_attention(step, 0)
-            if c >= 0:
-                conv_and_square(0, c)
-                conv_and_square(1, c)
-            if last:
-                variance(0, 1)
-                root(0, 1)
-            if step < N_CH:
-                banks[step, 1] = spread_attention(step, 1)
-            if step == 0:
-                turn_weights()
-            if c >= 0:
-                conv_and_square(2, c)
-            if last:
+            if 0 <= c < N_CH - 1:
+                ys = []
+                for m in range(N_TILES):
+                    ys.append(conv(m, c))
+                for m in range(N_TILES):
+                    add_to_sum(m, c)
+                    square(ys[m], m, c)
+            if c == N_CH - 1:
+                for m in range(N_TILES):
+                    y_last = conv(m, c)
+                    add_to_sum(m, c)
+                    square(y_last, m, c)
+                    if m == 1:
+                        variance(0, 1)
+                        root(0, 1)
                 gain_and_bias(0, 1)
                 variance(1, N_TILES)
             if step % 2 == 1 and 3 <= step <= 2 * CH_PER_IMAGE + 1:
                 node0_bank((step - 3) // 2)
+            if step < N_CH:
+                banks[step, 0] = spread_attention(step, 0)
+                banks[step, 1] = spread_attention(step, 1)
+            if step == 0:
+                turn_weights()
 
         groups = []
         for m in range(N_TILES):

@@ -35,6 +35,8 @@ WORK_0 = RAW_SLOTS * CHUNK_EL
 ARENA_EL = WORK_0 + WORK_SLOTS * 2 * CHUNK_EL
 REGION_EL = 2 * CHUNK_EL
 N_REGIONS = ARENA_EL // REGION_EL
+XG_SLOTS = 3
+XG_0 = ARENA_EL
 
 SUM_BANKS = (0, 1, 2)
 ATT_BANKS = (3, 4)
@@ -88,7 +90,7 @@ def tile_gnn_t_kernel(
         x_codes = keep.tile([P, N_CH, 2, CH], U32, align_bytes=64)
         x_scales = keep.tile([P, N_CH, 2, CH], U8, align_bytes=64)
         node_sb = keep.tile([P, N_TILES, BATCH, PIX], BF16)
-        arena = keep.tile([P, ARENA_EL], BF16, align_bytes=64)
+        arena = keep.tile([P, ARENA_EL + XG_SLOTS * CHUNK_EL], BF16, align_bytes=64)
         p0 = keep.tile([P, PIX], BF16)
         h0 = keep.tile([P, PIX], BF16)
 
@@ -112,7 +114,8 @@ def tile_gnn_t_kernel(
             return arena[:, WORK_0 + k * 2 * CHUNK_EL : WORK_0 + (k + 1) * 2 * CHUNK_EL]
 
         def grouped(s):
-            return work_slot(s + 1)[:, 0:CHUNK_EL]
+            k = s % XG_SLOTS
+            return arena[:, XG_0 + k * CHUNK_EL : XG_0 + (k + 1) * CHUNK_EL]
 
         def load_chunk(c):
             b, k = divmod(c, CH_PER_IMAGE)

@@ -38,6 +38,8 @@ N_REGIONS = ARENA_EL // REGION_EL
 XG_SLOTS = 3
 XG_0 = ARENA_EL
 
+NODE0_STEPS = (5, 7, 8, 9, 11, 13, 15, 17)
+
 SUM_BANKS = (0, 1, 2)
 ATT_BANKS = (3, 4)
 Y_BANKS = (5, 6, 7)
@@ -131,8 +133,6 @@ def tile_gnn_t_kernel(
         nc.sync.dma_start(out=par_rows[2:3, :], in_=gamma_l.rearrange("(m q) -> m q", q=P))
         nc.sync.dma_start(out=par_rows[3:5, :], in_=beta_u.rearrange("(m q) -> m q", q=P))
         nc.sync.dma_start(out=par_rows[5:6, :], in_=beta_l.rearrange("(m q) -> m q", q=P))
-        nc.sync.dma_start(out=p0[:], in_=p_nodes[0].rearrange("b c h w -> (b c) (h w)"))
-        nc.sync.dma_start(out=h0[:], in_=h_nodes[0].rearrange("b c h w -> (b c) (h w)"))
 
         att_t = next_bank(Y_BANKS, "y", [P, P], BF16)
         nc.tensor.transpose(att_t[:], att_rows[:], ident_bf[:])
@@ -160,25 +160,29 @@ def tile_gnn_t_kernel(
                 )
 
         acc = []
-        for m in range(N_TILES):
-            acc_m = psum.tile([P, SUM_W], F32, tag="bank%d" % SUM_BANKS[m], name="acc%d" % m)
-            acc.append(acc_m)
+        par_t = psum.tile([P, P], BF16, tag="bank%d" % SUM_BANKS[-1], name="par_t")
         ssq = keep.tile([P, N_TILES, N_CH], F32)
+
+        tie = const.tile([P, 1], U32)
+
+        def regroup_on_vector(s, lo, hi):
+            nc.vector.tensor_copy(
+                out=grouped(s).rearrange("p (c i t) -> p c t i", i=4, t=PACK)[:, lo // 4 : hi // 4],
+                in_=raw_slot(s)[:, :, lo:hi].rearrange("p t (c i) -> p c t i", i=4),
+            )
 
         def regroup(s):
             raw = raw_slot(s)
             xg = grouped(s).rearrange("p (w t) -> p w t", t=PACK)
-            s_end = S_PIX if s > 0 else CH // 4
-            g_start = S_PIX if s > 0 else 3 * CH // 4
+            s_end, g_start = {0: (CH // 4, 3 * CH // 4), 1: (S_PIX, S_PIX + 96)}.get(s, (S_PIX, S_PIX))
             nc.scalar.copy(
                 out=xg[:, 0:s_end, :].rearrange("p (c i) t -> p c t i", i=4),
                 in_=raw[:, :, 0:s_end].rearrange("p t (c i) -> p c t i", i=4),
             )
-            if g_start > s_end:
-                nc.vector.tensor_copy(
-                    out=xg[:, s_end:g_start, :].rearrange("p (c i) t -> p c t i", i=4),
-                    in_=raw[:, :, s_end:g_start].rearrange("p t (c i) -> p c t i", i=4),
-                )
+            if s == 0:
+                regroup_on_vector(s, s_end, g_start)
+            if s == 2:
+                nc.gpsimd.tensor_copy(out=tie[:], in_=w_codes[:, N_TILES - 1, 0:1])
             nc.gpsimd.tensor_scalar(
                 out=xg[:, g_start:CH, :],
                 in0=raw[:, :, g_start:CH].rearrange("p t w -> p w t"),
@@ -320,10 +324,17 @@ def tile_gnn_t_kernel(
         for step in range(N_CH + 3):
             if step < N_CH:
                 regroup(step)
-                if step + RAW_SLOTS < N_CH:
-                    load_chunk(step + RAW_SLOTS)
-                if step < N_TILES * BATCH * 2:
-                    load_node(step)
+            if step == 2:
+                nc.scalar.copy(
+                    out=par_mixed[:].rearrange("r (h j) -> r h j", j=2),
+                    in_=par_rows[:].rearrange("r (j h) -> r h j", j=2),
+                )
+                nc.tensor.transpose(par_t[:], par_mixed[:], ident_bf[:])
+            if step == 3:
+                nc.scalar.mul(out=par[:], in_=par_t[:, 0 : 2 * N_TILES], mul=0.5)
+                for m in range(N_TILES):
+                    acc_m = psum.tile([P, SUM_W], F32, tag="bank%d" % SUM_BANKS[m], name="acc%d" % m)
+                    acc.append(acc_m)
             c = step - 1
             if c == N_CH - 1:
                 quantise(c - 1)
@@ -337,17 +348,17 @@ def tile_gnn_t_kernel(
             if 0 <= c < N_CH - 2:
                 quantise(c)
             if step == 1:
+                regroup_on_vector(1, S_PIX, S_PIX + 96)
                 quantise_weights()
-                nc.vector.tensor_copy(
-                    out=par_mixed[:].rearrange("r (h j) -> r h j", j=2),
-                    in_=par_rows[:].rearrange("r (j h) -> r h j", j=2),
-                )
-            if step == 2:
-                par_t = next_bank(Y_BANKS, "y", [P, P], BF16)
-                nc.tensor.transpose(par_t[:], par_mixed[:], ident_bf[:])
-                nc.vector.tensor_scalar(
-                    out=par[:], in0=par_t[:, 0 : 2 * N_TILES], scalar1=0.5, scalar2=None, op0=ALU.mult
-                )
+            if step < N_CH:
+                if step + RAW_SLOTS < N_CH:
+                    load_chunk(step + RAW_SLOTS)
+                if step == 1:
+                    nc.sync.dma_start(out=p0[:], in_=p_nodes[0].rearrange("b c h w -> (b c) (h w)"))
+                if step == 2:
+                    nc.sync.dma_start(out=h0[:], in_=h_nodes[0].rearrange("b c h w -> (b c) (h w)"))
+                if 3 <= step < N_TILES * BATCH * 2 + 3:
+                    load_node(step - 3)
             c = step - 3
             if 0 <= c < N_CH - 1:
                 ys = []
@@ -366,8 +377,8 @@ def tile_gnn_t_kernel(
                         root(0, 1)
                 gain_and_bias(0, 1)
                 variance(1, N_TILES)
-            if step % 2 == 1 and 3 <= step <= 2 * CH_PER_IMAGE + 1:
-                node0_bank((step - 3) // 2)
+            if step in NODE0_STEPS:
+                node0_bank(NODE0_STEPS.index(step))
             if step < N_CH:
                 banks[step, 0] = spread_attention(step, 0)
                 banks[step, 1] = spread_attention(step, 1)

@@ -38,12 +38,12 @@ N_REGIONS = ARENA_EL // REGION_EL
 XG_SLOTS = 3
 XG_0 = ARENA_EL
 
-NODE0_STEPS = (5, 7, 8, 9, 11, 13, 15, 17)
+NODE0_STEPS = (5, 7, 8, 9, 11, 13, 14, 15)
 
 SUM_BANKS = (0, 1, 2)
 ATT_BANKS = (3, 4)
 Y_BANKS = (5, 6, 7)
-Z_BANKS = (3, 4, 5, 6, 7, 0, 1, 2)
+Z_BANKS = (3, 4, 6, 7, 5, 0, 1, 2)
 
 FLOPS = 2 * N_TILES * P * PACK * P * N_PIX
 BYTES = 2 * (7 * N_PIX * HID + N_PIX * HID + N_PIX * PACK * P + 2 * N_PIX + N_TILES * P * (PACK * P + 2)) + 4 * 7 * N_PIX * HID
@@ -161,7 +161,8 @@ def tile_gnn_t_kernel(
 
         acc = []
         par_t = psum.tile([P, P], BF16, tag="bank%d" % SUM_BANKS[-1], name="par_t")
-        ssq = keep.tile([P, N_TILES, N_CH], F32)
+        ssq = keep.tile([P, N_TILES, N_CH - 1], F32)
+        ssq_last = keep.tile([P, N_TILES], F32)
 
         tie = const.tile([P, 1], U32)
 
@@ -174,7 +175,7 @@ def tile_gnn_t_kernel(
         def regroup(s):
             raw = raw_slot(s)
             xg = grouped(s).rearrange("p (w t) -> p w t", t=PACK)
-            s_end, g_start = {0: (CH // 4, 3 * CH // 4), 1: (S_PIX, S_PIX + 96)}.get(s, (S_PIX, S_PIX))
+            s_end, g_start = {0: (3 * CH // 8, CH), 1: (S_PIX, S_PIX + 96)}.get(s, (S_PIX, S_PIX))
             nc.scalar.copy(
                 out=xg[:, 0:s_end, :].rearrange("p (c i) t -> p c t i", i=4),
                 in_=raw[:, :, 0:s_end].rearrange("p t (c i) -> p c t i", i=4),
@@ -183,14 +184,15 @@ def tile_gnn_t_kernel(
                 regroup_on_vector(s, s_end, g_start)
             if s == 2:
                 nc.gpsimd.tensor_copy(out=tie[:], in_=w_codes[:, N_TILES - 1, 0:1])
-            nc.gpsimd.tensor_scalar(
-                out=xg[:, g_start:CH, :],
-                in0=raw[:, :, g_start:CH].rearrange("p t w -> p w t"),
-                scalar1=1.0,
-                scalar2=0.0,
-                op0=ALU.mult,
-                op1=ALU.add,
-            )
+            if g_start < CH:
+                nc.gpsimd.tensor_scalar(
+                    out=xg[:, g_start:CH, :],
+                    in0=raw[:, :, g_start:CH].rearrange("p t w -> p w t"),
+                    scalar1=1.0,
+                    scalar2=0.0,
+                    op0=ALU.mult,
+                    op1=ALU.add,
+                )
 
         def spread_attention(c, i):
             bank = next_bank(ATT_BANKS, "att", [P, CH], F32)
@@ -259,7 +261,13 @@ def tile_gnn_t_kernel(
 
         def square(y, m, c):
             junk = junk_pool.tile([P, CH], BF16, name="junk")
-            nc.scalar.activation(out=junk[:], in_=y[:], func=ACT.Square, accum_out=ssq[:, m, c : c + 1])
+            nc.scalar.activation(
+                out=junk[:],
+                in_=y[:],
+                func=ACT.Square,
+                scale=N_PIX**-0.5,
+                accum_out=ssq[:, m, c : c + 1] if c < N_CH - 1 else ssq_last[:, m : m + 1],
+            )
 
         def load_node(k):
             m, rest = divmod(k, 2 * BATCH)
@@ -272,53 +280,92 @@ def tile_gnn_t_kernel(
         par_mixed = const.tile([P, P], BF16)
         par = keep.tile([P, 2 * N_TILES], F32)
         sums = keep.tile([P, N_TILES], F32)
-        neg_mean = keep.tile([P, N_TILES], F32)
         mean_sq = keep.tile([P, N_TILES], F32)
-        ssq_sum = keep.tile([P, N_TILES], F32)
-        var = keep.tile([P, N_TILES], F32)
+        part_sq = keep.tile([P, N_TILES], F32)
+        part_eps = keep.tile([P, N_TILES], F32)
+        rest = keep.tile([P, N_TILES], F32)
+        shift = keep.tile([P, N_TILES], F32)
         var_eps = keep.tile([P, N_TILES], F32)
         std = keep.tile([P, N_TILES], F32)
         rstd = keep.tile([P, N_TILES], F32)
         half_gain = keep.tile([P, N_TILES], F32)
         half_bias = keep.tile([P, N_TILES], F32)
+        eps = const.tile([P, 1], F32)
+        nc.vector.tensor_scalar(out=eps[:], in0=one[:], scalar1=EPS, scalar2=None, op0=ALU.mult)
 
-        def variance(lo, hi):
-            for m in range(lo, hi):
-                nc.vector.tensor_reduce(out=sums[:, m : m + 1], in_=acc[m][:], axis=AX.X, op=ALU.add)
-            nc.vector.tensor_scalar(
-                out=neg_mean[:, lo:hi], in0=sums[:, lo:hi], scalar1=-1.0 / N_PIX, scalar2=None, op0=ALU.mult
-            )
-            nc.vector.tensor_tensor(
-                out=mean_sq[:, lo:hi], in0=neg_mean[:, lo:hi], in1=neg_mean[:, lo:hi], op=ALU.mult
-            )
-            nc.vector.tensor_reduce(out=ssq_sum[:, lo:hi], in_=ssq[:, lo:hi, :], axis=AX.X, op=ALU.add)
+        def total(m):
+            nc.vector.tensor_reduce(out=sums[:, m : m + 1], in_=acc[m][:], axis=AX.X, op=ALU.add)
+
+        def squares_so_far():
+            nc.vector.tensor_reduce(out=part_sq[:], in_=ssq[:], axis=AX.X, op=ALU.add)
+            nc.vector.tensor_scalar(out=part_eps[:], in0=part_sq[:], scalar1=EPS, scalar2=None, op0=ALU.add)
+
+        def mean_square(m):
             nc.vector.scalar_tensor_tensor(
-                out=var[:, lo:hi],
-                in0=ssq_sum[:, lo:hi],
-                scalar=1.0 / N_PIX,
-                in1=mean_sq[:, lo:hi],
+                out=mean_sq[:, m : m + 1],
+                in0=sums[:, m : m + 1],
+                scalar=1.0 / (N_PIX * N_PIX),
+                in1=sums[:, m : m + 1],
                 op0=ALU.mult,
-                op1=ALU.subtract,
+                op1=ALU.mult,
+            )
+
+        def prepare(m):
+            nc.vector.tensor_tensor(
+                out=rest[:, m : m + 1], in0=part_eps[:, m : m + 1], in1=mean_sq[:, m : m + 1], op=ALU.subtract
+            )
+            nc.vector.scalar_tensor_tensor(
+                out=shift[:, m : m + 1],
+                in0=sums[:, m : m + 1],
+                scalar=-1.0 / N_PIX,
+                in1=par[:, m : m + 1],
+                op0=ALU.mult,
+                op1=ALU.mult,
+            )
+
+        def variance(m):
+            nc.vector.tensor_scalar(
+                out=var_eps[:, m : m + 1],
+                in0=ssq_last[:, m : m + 1],
+                scalar1=rest[:, m : m + 1],
+                scalar2=eps[:],
+                op0=ALU.add,
+                op1=ALU.max,
+            )
+
+        def root(m):
+            nc.scalar.activation(out=std[:, m : m + 1], in_=var_eps[:, m : m + 1], func=ACT.Sqrt)
+
+        def reciprocal(m):
+            nc.vector.reciprocal(out=rstd[:, m : m + 1], in_=std[:, m : m + 1])
+
+        def gain_and_bias(m):
+            nc.vector.tensor_tensor(
+                out=half_gain[:, m : m + 1], in0=rstd[:, m : m + 1], in1=par[:, m : m + 1], op=ALU.mult
             )
             nc.vector.tensor_scalar(
-                out=var_eps[:, lo:hi], in0=var[:, lo:hi], scalar1=0.0, scalar2=EPS, op0=ALU.max, op1=ALU.add
+                out=half_bias[:, m : m + 1],
+                in0=rstd[:, m : m + 1],
+                scalar1=shift[:, m : m + 1],
+                scalar2=par[:, N_TILES + m : N_TILES + m + 1],
+                op0=ALU.mult,
+                op1=ALU.add,
             )
 
-        def root(lo, hi):
-            nc.scalar.activation(out=std[:, lo:hi], in_=var_eps[:, lo:hi], func=ACT.Sqrt)
-
-        def gain_and_bias(lo, hi):
-            nc.vector.reciprocal(out=rstd[:, lo:hi], in_=std[:, lo:hi])
-            nc.vector.tensor_tensor(out=half_gain[:, lo:hi], in0=rstd[:, lo:hi], in1=par[:, lo:hi], op=ALU.mult)
-            for m in range(lo, hi):
-                nc.vector.scalar_tensor_tensor(
-                    out=half_bias[:, m : m + 1],
-                    in0=neg_mean[:, m : m + 1],
-                    scalar=half_gain[:, m : m + 1],
-                    in1=par[:, N_TILES + m : N_TILES + m + 1],
-                    op0=ALU.mult,
-                    op1=ALU.add,
-                )
+        small_steps = {
+            0: (prepare, 1),
+            1: (variance, 1),
+            2: (total, 2),
+            3: (root, 1),
+            4: (reciprocal, 1),
+            5: (gain_and_bias, 1),
+            9: (mean_square, 2),
+            10: (prepare, 2),
+            11: (variance, 2),
+            13: (root, 2),
+            14: (reciprocal, 2),
+            15: (gain_and_bias, 2),
+        }
 
         banks = {}
         for step in range(N_CH + 3):
@@ -368,19 +415,27 @@ def tile_gnn_t_kernel(
                     add_to_sum(m, c)
                     square(ys[m], m, c)
             if c == N_CH - 1:
-                for m in range(N_TILES):
-                    y_last = conv(m, c)
+                squares_so_far()
+                for m in range(2):
                     add_to_sum(m, c)
-                    square(y_last, m, c)
+                    y_last = conv(m, c)
                     if m == 1:
-                        variance(0, 1)
-                        root(0, 1)
-                gain_and_bias(0, 1)
-                variance(1, N_TILES)
+                        root(0)
+                    square(y_last, m, c)
+                    if m == 0:
+                        total(0)
+                        mean_square(0)
+                        prepare(0)
+                        variance(0)
+                reciprocal(0)
+                gain_and_bias(0)
+                total(1)
+                mean_square(1)
+            if step < N_CH:
+                banks[step, 0] = spread_attention(step, 0)
             if step in NODE0_STEPS:
                 node0_bank(NODE0_STEPS.index(step))
             if step < N_CH:
-                banks[step, 0] = spread_attention(step, 0)
                 banks[step, 1] = spread_attention(step, 1)
             if step == 0:
                 turn_weights()
@@ -397,6 +452,7 @@ def tile_gnn_t_kernel(
                 for n in sizes:
                     groups.append((m, b, k0, n))
                     k0 += n
+        n_added = 0
         for g, (m, b, k0, n) in enumerate(groups):
             r = g % N_REGIONS
             t = arena[:, r * REGION_EL : r * REGION_EL + 2 * n * CH].bitcast(F32)
@@ -411,8 +467,9 @@ def tile_gnn_t_kernel(
                     scale=half_gain[:, m : m + 1],
                     bias=half_bias[:, m : m + 1],
                 )
-                if k % 2 == 1 or k == n - 1 or g >= len(groups) - 3:
-                    a = k - 1 if (k % 2 == 1 and g < len(groups) - 3) else k
+                alone = g < 3 or g >= len(groups) - 3
+                if alone or k % 2 == 1 or k == n - 1:
+                    a = k - 1 if (k % 2 == 1 and not alone) else k
                     nc.vector.scalar_tensor_tensor(
                         out=t[:, a * CH : (k + 1) * CH],
                         in0=node_sb[:, m, b, (k0 + a) * CH : (k0 + k + 1) * CH],
@@ -421,11 +478,16 @@ def tile_gnn_t_kernel(
                         op0=ALU.mult,
                         op1=ALU.add,
                     )
+                    if n_added in small_steps:
+                        step_of, tile = small_steps[n_added]
+                        step_of(tile)
+                    n_added += 1
+            if g == 0:
+                add_to_sum(2, N_CH - 1)
+                y_last = conv(2, N_CH - 1)
+                square(y_last, 2, N_CH - 1)
             for j in range(2):
                 nc.sync.dma_start(
                     out=out[1 + 2 * m + j, b].rearrange("c h w -> c (h w)")[:, cols],
                     in_=t[j:P:2, :],
                 )
-            if g == 1:
-                root(1, N_TILES)
-                gain_and_bias(1, N_TILES)

@@ -24,8 +24,11 @@ N_PIX = BATCH * PIX
 N_TILES = 3
 BRANCH = (0, 0, 1)
 EPS = 1e-5
-G_PIX = 224
+G_PIX = 256
 S_PIX = CH - G_PIX
+V_PIX = 96
+HALF = CH // 2
+HEAD_G_PIX = 128
 SUM_W = 256
 
 CHUNK_EL = PACK * CH
@@ -43,7 +46,7 @@ NODE0_STEPS = (5, 7, 8, 9, 11, 13, 14, 15)
 SUM_BANKS = (0, 1, 2)
 ATT_BANKS = (3, 4)
 Y_BANKS = (5, 6, 7)
-Z_BANKS = (3, 4, 6, 7, 5, 0, 1, 2)
+Z_BANKS = (3, 4, 6, 7, 5, 0, 1)
 
 FLOPS = 2 * N_TILES * P * PACK * P * N_PIX
 BYTES = 2 * (7 * N_PIX * HID + N_PIX * HID + N_PIX * PACK * P + 2 * N_PIX + N_TILES * P * (PACK * P + 2)) + 4 * 7 * N_PIX * HID
@@ -124,7 +127,8 @@ def tile_gnn_t_kernel(
             nc.sync.dma_start(out=raw_slot(c), in_=xp_rows[b, :, :, k * CH : (k + 1) * CH])
 
         nc.sync.dma_start(out=att_rows[:], in_=att_src)
-        load_chunk(0)
+        for lo in (0, HALF):
+            nc.sync.dma_start(out=raw_slot(0)[:, :, lo : lo + HALF], in_=xp_rows[0, :, :, lo : lo + HALF])
         nc.sync.dma_start(out=w_rows[:, 0:2, :], in_=Wu.rearrange("(m q) c -> q m c", q=P))
         nc.sync.dma_start(out=w_rows[:, 2, :], in_=Wl)
         for c in range(1, RAW_SLOTS):
@@ -166,33 +170,31 @@ def tile_gnn_t_kernel(
 
         tie = const.tile([P, 1], U32)
 
-        def regroup_on_vector(s, lo, hi):
-            nc.vector.tensor_copy(
+        def regroup_on(copy, s, lo, hi):
+            copy(
                 out=grouped(s).rearrange("p (c i t) -> p c t i", i=4, t=PACK)[:, lo // 4 : hi // 4],
                 in_=raw_slot(s)[:, :, lo:hi].rearrange("p t (c i) -> p c t i", i=4),
             )
 
         def regroup(s):
-            raw = raw_slot(s)
-            xg = grouped(s).rearrange("p (w t) -> p w t", t=PACK)
-            s_end, g_start = {0: (3 * CH // 8, CH), 1: (S_PIX, S_PIX + 96)}.get(s, (S_PIX, S_PIX))
-            nc.scalar.copy(
-                out=xg[:, 0:s_end, :].rearrange("p (c i) t -> p c t i", i=4),
-                in_=raw[:, :, 0:s_end].rearrange("p t (c i) -> p c t i", i=4),
-            )
             if s == 0:
-                regroup_on_vector(s, s_end, g_start)
+                regroup_on(nc.scalar.copy, 0, 0, V_PIX)
+                regroup_on(nc.vector.tensor_copy, 0, V_PIX, HALF)
+                regroup_on(nc.scalar.copy, 0, HALF, CH)
+                return
+            s_end = CH - HEAD_G_PIX if s in (2, 3) else S_PIX
+            g_start = s_end + V_PIX if s == 1 else s_end
+            regroup_on(nc.scalar.copy, s, 0, s_end)
             if s == 2:
                 nc.gpsimd.tensor_copy(out=tie[:], in_=w_codes[:, N_TILES - 1, 0:1])
-            if g_start < CH:
-                nc.gpsimd.tensor_scalar(
-                    out=xg[:, g_start:CH, :],
-                    in0=raw[:, :, g_start:CH].rearrange("p t w -> p w t"),
-                    scalar1=1.0,
-                    scalar2=0.0,
-                    op0=ALU.mult,
-                    op1=ALU.add,
-                )
+            nc.gpsimd.tensor_scalar(
+                out=grouped(s).rearrange("p (w t) -> p w t", t=PACK)[:, g_start:CH, :],
+                in0=raw_slot(s)[:, :, g_start:CH].rearrange("p t w -> p w t"),
+                scalar1=1.0,
+                scalar2=0.0,
+                op0=ALU.mult,
+                op1=ALU.add,
+            )
 
         def spread_attention(c, i):
             bank = next_bank(ATT_BANKS, "att", [P, CH], F32)
@@ -205,17 +207,17 @@ def tile_gnn_t_kernel(
                 )
             return bank
 
-        def weigh(c, i, bank):
+        def weigh(c, i, bank, lo=0, hi=CH):
             nc.vector.tensor_tensor(
-                out=work_slot(c)[:, i * CHUNK_EL : (i + 1) * CHUNK_EL].rearrange(
+                out=work_slot(c)[:, i * CHUNK_EL + lo * PACK : i * CHUNK_EL + hi * PACK].rearrange(
                     "p (w h e) -> p w h e", h=2, e=2
                 ),
-                in0=grouped(c).rearrange("p (w h e) -> p w h e", h=2, e=2),
-                in1=bank[:]
+                in0=grouped(c)[:, lo * PACK : hi * PACK].rearrange("p (w h e) -> p w h e", h=2, e=2),
+                in1=bank[:, lo:hi]
                 .bitcast(BF16)
                 .rearrange("p (w e) -> p w e", e=2)
                 .unsqueeze(2)
-                .to_broadcast([P, CH, 2, 2]),
+                .to_broadcast([P, hi - lo, 2, 2]),
                 op=ALU.mult,
             )
 
@@ -385,7 +387,10 @@ def tile_gnn_t_kernel(
             c = step - 1
             if c == N_CH - 1:
                 quantise(c - 1)
-            if 0 <= c < N_CH:
+            for lo in (0, HALF) if c == 0 else ():
+                weigh(c, 0, banks[c, 0], lo, lo + HALF)
+                weigh(c, 1, banks[c, 1], lo, lo + HALF)
+            if 0 < c < N_CH:
                 weigh(c, 0, banks[c, 0])
                 weigh(c, 1, banks[c, 1])
             if c == N_CH - 1:
@@ -395,7 +400,7 @@ def tile_gnn_t_kernel(
             if 0 <= c < N_CH - 2:
                 quantise(c)
             if step == 1:
-                regroup_on_vector(1, S_PIX, S_PIX + 96)
+                regroup_on(nc.vector.tensor_copy, 1, S_PIX, S_PIX + V_PIX)
                 quantise_weights()
             if step < N_CH:
                 if step + RAW_SLOTS < N_CH:

@@ -144,6 +144,16 @@ def tile_gnn_t_kernel(
         nc.vector.tensor_copy(out=att_pairs[:], in_=att_t[:].unsqueeze(2).to_broadcast([P, P, 2]))
         att_words = att_pairs[:].rearrange("q r e -> q (r e)").bitcast(F32)
 
+        first_att = next_bank(ATT_BANKS, "att", [P, CH, 2], BF16)
+        for s in range(CH // P):
+            nc.tensor.matmul(
+                out=first_att[:, s * P : (s + 1) * P, :],
+                lhsT=ident_bf[:, s : s + 1].to_broadcast([P, P]),
+                rhs=att_rows[:].unsqueeze(2).to_broadcast([P, P, 2]),
+                start=True,
+                stop=True,
+            )
+
         w_grouped = const.tile([P, N_TILES, PACK * P], BF16, align_bytes=64)
 
         def turn_weights():
@@ -205,7 +215,7 @@ def tile_gnn_t_kernel(
                     att_words[:, r : r + 1].to_broadcast([P, P]),
                     ident_f32[:],
                 )
-            return bank
+            return bank[:].bitcast(BF16).rearrange("p (w e) -> p w e", e=2)
 
         def weigh(c, i, bank, lo=0, hi=CH):
             nc.vector.tensor_tensor(
@@ -213,11 +223,7 @@ def tile_gnn_t_kernel(
                     "p (w h e) -> p w h e", h=2, e=2
                 ),
                 in0=grouped(c)[:, lo * PACK : hi * PACK].rearrange("p (w h e) -> p w h e", h=2, e=2),
-                in1=bank[:, lo:hi]
-                .bitcast(BF16)
-                .rearrange("p (w e) -> p w e", e=2)
-                .unsqueeze(2)
-                .to_broadcast([P, hi - lo, 2, 2]),
+                in1=bank[:, lo:hi, :].unsqueeze(2).to_broadcast([P, hi - lo, 2, 2]),
                 op=ALU.mult,
             )
 
@@ -300,6 +306,8 @@ def tile_gnn_t_kernel(
 
         def squares_so_far():
             nc.vector.tensor_reduce(out=part_sq[:], in_=ssq[:], axis=AX.X, op=ALU.add)
+
+        def add_eps():
             nc.vector.tensor_scalar(out=part_eps[:], in0=part_sq[:], scalar1=EPS, scalar2=None, op0=ALU.add)
 
         def mean_square(m):
@@ -420,7 +428,6 @@ def tile_gnn_t_kernel(
                     add_to_sum(m, c)
                     square(ys[m], m, c)
             if c == N_CH - 1:
-                squares_so_far()
                 for m in range(2):
                     add_to_sum(m, c)
                     y_last = conv(m, c)
@@ -429,14 +436,18 @@ def tile_gnn_t_kernel(
                     square(y_last, m, c)
                     if m == 0:
                         total(0)
+                        squares_so_far()
                         mean_square(0)
+                        add_eps()
                         prepare(0)
                         variance(0)
                 reciprocal(0)
                 gain_and_bias(0)
                 total(1)
                 mean_square(1)
-            if step < N_CH:
+            if step == 0:
+                banks[0, 0] = first_att[:]
+            elif step < N_CH:
                 banks[step, 0] = spread_attention(step, 0)
             if step in NODE0_STEPS:
                 node0_bank(NODE0_STEPS.index(step))

@@ -28,6 +28,7 @@ G_PIX = 256
 S_PIX = CH - G_PIX
 V_PIX = 96
 HALF = CH // 2
+V1_PIX = 96
 HEAD_G_PIX = 128
 SUM_W = 256
 
@@ -129,9 +130,10 @@ def tile_gnn_t_kernel(
         nc.sync.dma_start(out=att_rows[:], in_=att_src)
         for lo in (0, HALF):
             nc.sync.dma_start(out=raw_slot(0)[:, :, lo : lo + HALF], in_=xp_rows[0, :, :, lo : lo + HALF])
+        load_chunk(1)
         nc.sync.dma_start(out=w_rows[:, 0:2, :], in_=Wu.rearrange("(m q) c -> q m c", q=P))
         nc.sync.dma_start(out=w_rows[:, 2, :], in_=Wl)
-        for c in range(1, RAW_SLOTS):
+        for c in range(2, RAW_SLOTS):
             load_chunk(c)
         nc.sync.dma_start(out=par_rows[0:2, :], in_=gamma_u.rearrange("(m q) -> m q", q=P))
         nc.sync.dma_start(out=par_rows[2:3, :], in_=gamma_l.rearrange("(m q) -> m q", q=P))
@@ -178,7 +180,6 @@ def tile_gnn_t_kernel(
         ssq = keep.tile([P, N_TILES, N_CH - 1], F32)
         ssq_last = keep.tile([P, N_TILES], F32)
 
-        tie = const.tile([P, 1], U32)
 
         def regroup_on(copy, s, lo, hi):
             copy(
@@ -193,10 +194,8 @@ def tile_gnn_t_kernel(
                 regroup_on(nc.scalar.copy, 0, HALF, CH)
                 return
             s_end = CH - HEAD_G_PIX if s in (2, 3) else S_PIX
-            g_start = s_end + V_PIX if s == 1 else s_end
+            g_start = s_end
             regroup_on(nc.scalar.copy, s, 0, s_end)
-            if s == 2:
-                nc.gpsimd.tensor_copy(out=tie[:], in_=w_codes[:, N_TILES - 1, 0:1])
             nc.gpsimd.tensor_scalar(
                 out=grouped(s).rearrange("p (w t) -> p w t", t=PACK)[:, g_start:CH, :],
                 in0=raw_slot(s)[:, :, g_start:CH].rearrange("p t w -> p w t"),
@@ -379,19 +378,13 @@ def tile_gnn_t_kernel(
 
         banks = {}
         for step in range(N_CH + 3):
-            if step < N_CH:
-                regroup(step)
-            if step == 2:
-                nc.scalar.copy(
-                    out=par_mixed[:].rearrange("r (h j) -> r h j", j=2),
-                    in_=par_rows[:].rearrange("r (j h) -> r h j", j=2),
-                )
-                nc.tensor.transpose(par_t[:], par_mixed[:], ident_bf[:])
             if step == 3:
                 nc.scalar.mul(out=par[:], in_=par_t[:, 0 : 2 * N_TILES], mul=0.5)
                 for m in range(N_TILES):
                     acc_m = psum.tile([P, SUM_W], F32, tag="bank%d" % SUM_BANKS[m], name="acc%d" % m)
                     acc.append(acc_m)
+            if step < N_CH:
+                regroup(step)
             c = step - 1
             if c == N_CH - 1:
                 quantise(c - 1)
@@ -405,11 +398,10 @@ def tile_gnn_t_kernel(
                 quantise_branch(c, 0)
                 quantise_branch(c, 1)
             c = step - 2
+            if c == 0:
+                quantise_weights()
             if 0 <= c < N_CH - 2:
                 quantise(c)
-            if step == 1:
-                regroup_on(nc.vector.tensor_copy, 1, S_PIX, S_PIX + V_PIX)
-                quantise_weights()
             if step < N_CH:
                 if step + RAW_SLOTS < N_CH:
                     load_chunk(step + RAW_SLOTS)
@@ -453,8 +445,14 @@ def tile_gnn_t_kernel(
                 node0_bank(NODE0_STEPS.index(step))
             if step < N_CH:
                 banks[step, 1] = spread_attention(step, 1)
-            if step == 0:
+            if step == 1:
                 turn_weights()
+            if step == 2:
+                nc.scalar.copy(
+                    out=par_mixed[:].rearrange("r (h j) -> r h j", j=2),
+                    in_=par_rows[:].rearrange("r (j h) -> r h j", j=2),
+                )
+                nc.tensor.transpose(par_t[:], par_mixed[:], ident_bf[:])
 
         groups = []
         for m in range(N_TILES):

from contextlib import ExitStack

import concourse.mybir as mybir
from concourse.masks import make_identity

F32 = mybir.dt.float32
BF16 = mybir.dt.bfloat16
U32 = mybir.dt.uint32
U8 = mybir.dt.uint8
FP8X4 = mybir.dt.float8_e4m3fn_x4
ALU = mybir.AluOpType
ACT = mybir.ActivationFunctionType
AX = mybir.AxisListType

P = 128
PACK = 4
BATCH = 2
HID = 64
PIX = 4096
CH = 512
CH_PER_IMAGE = PIX // CH
N_CH = BATCH * CH_PER_IMAGE
N_PIX = BATCH * PIX
N_TILES = 3
BRANCH = (0, 0, 1)
EPS = 1e-5
G_PIX = 256
S_PIX = CH - G_PIX
V_PIX = 96
HALF = CH // 2
V1_PIX = 96
HEAD_G_PIX = 128
SUM_W = 256

CHUNK_EL = PACK * CH
RAW_SLOTS = 4
WORK_SLOTS = 4
WORK_0 = RAW_SLOTS * CHUNK_EL
ARENA_EL = WORK_0 + WORK_SLOTS * 2 * CHUNK_EL
REGION_EL = 2 * CHUNK_EL
N_REGIONS = ARENA_EL // REGION_EL
XG_SLOTS = 3
XG_0 = ARENA_EL

NODE0_STEPS = (5, 7, 8, 9, 11, 13, 14, 15)

SUM_BANKS = (0, 1, 2)
ATT_BANKS = (3, 4)
Y_BANKS = (5, 6, 7)
Z_BANKS = (3, 4, 6, 7, 5, 0, 1)

FLOPS = 2 * N_TILES * P * PACK * P * N_PIX
BYTES = 2 * (7 * N_PIX * HID + N_PIX * HID + N_PIX * PACK * P + 2 * N_PIX + N_TILES * P * (PACK * P + 2)) + 4 * 7 * N_PIX * HID


def tile_gnn_t_kernel(
    tc, p_nodes, h_nodes, f_nodes, xp, h_att, Wu, Wl, gamma_u, beta_u, gamma_l, beta_l, out
):
    nc = tc.nc
    with ExitStack() as ctx:
        ctx.enter_context(tc.manual_schedule())
        const = ctx.enter_context(tc.tile_pool(name="const", bufs=1))
        keep = ctx.enter_context(tc.tile_pool(name="keep", bufs=1))
        junk_pool = ctx.enter_context(tc.tile_pool(name="junk", bufs=4))
        o0_pool = ctx.enter_context(tc.tile_pool(name="o0", bufs=3))
        psum = ctx.enter_context(tc.psum_pool(name="psum", bufs=1))

        taken = {"att": 0, "y": 0, "z": 0}

        def next_bank(ring, key, shape, dtype):
            k = ring[taken[key] % len(ring)]
            taken[key] = taken[key] + 1
            got = psum.tile(shape, dtype, tag="bank%d" % k, name="bank%d" % k)
            return got

        xp_rows = xp.rearrange("b (p j) h w -> b p j (h w)", j=PACK)
        att_src = h_att[1:3].rearrange("i b o (hh hl) w -> (i b o hh) (hl w)", hl=2)

        att_rows = const.tile([P, P], BF16)
        w_rows = const.tile([P, N_TILES, PACK * P], BF16)
        par_rows = const.tile([P, P], BF16)
        nc.vector.memset(par_rows[:], 0.0)

        ident_bf = const.tile([P, P], BF16)
        make_identity(nc, ident_bf[:])
        ident_f32 = const.tile([P, P], F32)
        make_identity(nc, ident_f32[:])

        one = const.tile([P, 1], F32)
        nc.vector.memset(one[:], 1.0)
        warm = const.tile([P, 1], F32)
        nc.scalar.activation(out=warm[:], in_=one[:], func=ACT.Sqrt)

        w_codes = keep.tile([P, N_TILES, P], U32, align_bytes=64)
        w_scales = keep.tile([P, N_TILES, P], U8, align_bytes=64)
        x_codes = keep.tile([P, N_CH, 2, CH], U32, align_bytes=64)
        x_scales = keep.tile([P, N_CH, 2, CH], U8, align_bytes=64)
        node_sb = keep.tile([P, N_TILES, BATCH, PIX], BF16)
        arena = keep.tile([P, ARENA_EL + XG_SLOTS * CHUNK_EL], BF16, align_bytes=64)
        p0 = keep.tile([P, PIX], BF16)
        h0 = keep.tile([P, PIX], BF16)

        def conv_pass(dst, m, c, lo, hi, start, stop):
            nc.tensor.matmul_mx(
                out=dst,
                lhsT=w_codes[:, m, :].bitcast(FP8X4),
                lhsT_scale=w_scales[:, m, :],
                rhs=x_codes[:, c, BRANCH[m], lo:hi].bitcast(FP8X4),
                rhs_scale=x_scales[:, c, BRANCH[m], lo:hi],
                start=start,
                stop=stop,
            )

        def raw_slot(s):
            k = s % RAW_SLOTS
            return arena[:, k * CHUNK_EL : (k + 1) * CHUNK_EL].rearrange("p (t w) -> p t w", t=PACK)

        def work_slot(c):
            k = c % WORK_SLOTS
            return arena[:, WORK_0 + k * 2 * CHUNK_EL : WORK_0 + (k + 1) * 2 * CHUNK_EL]

        def grouped(s):
            k = s % XG_SLOTS
            return arena[:, XG_0 + k * CHUNK_EL : XG_0 + (k + 1) * CHUNK_EL]

        def load_chunk(c):
            b, k = divmod(c, CH_PER_IMAGE)
            nc.sync.dma_start(out=raw_slot(c), in_=xp_rows[b, :, :, k * CH : (k + 1) * CH])

        nc.sync.dma_start(out=att_rows[:], in_=att_src)
        for lo in (0, HALF):
            nc.sync.dma_start(out=raw_slot(0)[:, :, lo : lo + HALF], in_=xp_rows[0, :, :, lo : lo + HALF])
        load_chunk(1)
        nc.sync.dma_start(out=w_rows[:, 0:2, :], in_=Wu.rearrange("(m q) c -> q m c", q=P))
        nc.sync.dma_start(out=w_rows[:, 2, :], in_=Wl)
        for c in range(2, RAW_SLOTS):
            load_chunk(c)
        nc.sync.dma_start(out=par_rows[0:2, :], in_=gamma_u.rearrange("(m q) -> m q", q=P))
        nc.sync.dma_start(out=par_rows[2:3, :], in_=gamma_l.rearrange("(m q) -> m q", q=P))
        nc.sync.dma_start(out=par_rows[3:5, :], in_=beta_u.rearrange("(m q) -> m q", q=P))
        nc.sync.dma_start(out=par_rows[5:6, :], in_=beta_l.rearrange("(m q) -> m q", q=P))

        att_t = next_bank(Y_BANKS, "y", [P, P], BF16)
        nc.tensor.transpose(att_t[:], att_rows[:], ident_bf[:])
        att_pairs = const.tile([P, P, 2], BF16)
        nc.vector.tensor_copy(out=att_pairs[:], in_=att_t[:].unsqueeze(2).to_broadcast([P, P, 2]))
        att_words = att_pairs[:].rearrange("q r e -> q (r e)").bitcast(F32)

        first_att = next_bank(ATT_BANKS, "att", [P, CH, 2], BF16)
        for s in range(CH // P):
            nc.tensor.matmul(
                out=first_att[:, s * P : (s + 1) * P, :],
                lhsT=ident_bf[:, s : s + 1].to_broadcast([P, P]),
                rhs=att_rows[:].unsqueeze(2).to_broadcast([P, P, 2]),
                start=True,
                stop=True,
            )

        w_grouped = const.tile([P, N_TILES, PACK * P], BF16, align_bytes=64)

        def turn_weights():
            for m in range(N_TILES):
                w_words = w_rows[:, m, :].bitcast(F32)
                w_t = next_bank(Y_BANKS, "y", [P, 2, P], F32)
                for u in range(2):
                    nc.tensor.transpose(w_t[:, u, :], w_words[:, u : 2 * P : 2], ident_f32[:])
                nc.scalar.copy(
                    out=w_grouped[:, m, :].bitcast(F32).rearrange("p (h j u) -> p h j u", j=2, u=2),
                    in_=w_t[:].rearrange("p u (j h) -> p h j u", j=2),
                )

        def quantise_weights():
            for m in range(N_TILES):
                nc.vector.quantize_mx(
                    out=w_codes[:, m, :].bitcast(FP8X4), scales=w_scales[:, m, :], in_=w_grouped[:, m, :]
                )

        acc = []
        par_t = psum.tile([P, P], BF16, tag="bank%d" % SUM_BANKS[-1], name="par_t")
        ssq = keep.tile([P, N_TILES, N_CH - 1], F32)
        ssq_last = keep.tile([P, N_TILES], F32)


        def regroup_on(copy, s, lo, hi):
            copy(
                out=grouped(s).rearrange("p (c i t) -> p c t i", i=4, t=PACK)[:, lo // 4 : hi // 4],
                in_=raw_slot(s)[:, :, lo:hi].rearrange("p t (c i) -> p c t i", i=4),
            )

        def regroup(s):
            if s == 0:
                regroup_on(nc.scalar.copy, 0, 0, V_PIX)
                regroup_on(nc.vector.tensor_copy, 0, V_PIX, HALF)
                regroup_on(nc.scalar.copy, 0, HALF, CH)
                return
            s_end = CH - HEAD_G_PIX if s in (2, 3) else S_PIX
            g_start = s_end
            regroup_on(nc.scalar.copy, s, 0, s_end)
            nc.gpsimd.tensor_scalar(
                out=grouped(s).rearrange("p (w t) -> p w t", t=PACK)[:, g_start:CH, :],
                in0=raw_slot(s)[:, :, g_start:CH].rearrange("p t w -> p w t"),
                scalar1=1.0,
                scalar2=0.0,
                op0=ALU.mult,
                op1=ALU.add,
            )

        def spread_attention(c, i):
            bank = next_bank(ATT_BANKS, "att", [P, CH], F32)
            for s in range(CH // P):
                r = i * (N_PIX // P) + c * (CH // P) + s
                nc.tensor.transpose(
                    bank[:, s * P : (s + 1) * P],
                    att_words[:, r : r + 1].to_broadcast([P, P]),
                    ident_f32[:],
                )
            return bank[:].bitcast(BF16).rearrange("p (w e) -> p w e", e=2)

        def weigh(c, i, bank, lo=0, hi=CH):
            nc.vector.tensor_tensor(
                out=work_slot(c)[:, i * CHUNK_EL + lo * PACK : i * CHUNK_EL + hi * PACK].rearrange(
                    "p (w h e) -> p w h e", h=2, e=2
                ),
                in0=grouped(c)[:, lo * PACK : hi * PACK].rearrange("p (w h e) -> p w h e", h=2, e=2),
                in1=bank[:, lo:hi, :].unsqueeze(2).to_broadcast([P, hi - lo, 2, 2]),
                op=ALU.mult,
            )

        def quantise(c):
            nc.vector.quantize_mx(
                out=x_codes[:, c, :, :].rearrange("p i w -> p (i w)").bitcast(FP8X4),
                scales=x_scales[:, c, :, :].rearrange("p i w -> p (i w)"),
                in_=work_slot(c),
            )

        def quantise_branch(c, i):
            nc.vector.quantize_mx(
                out=x_codes[:, c, i, :].bitcast(FP8X4),
                scales=x_scales[:, c, i, :],
                in_=work_slot(c)[:, i * CHUNK_EL : (i + 1) * CHUNK_EL],
            )

        def node0_bank(i):
            cols = slice(i * CH, (i + 1) * CH)
            both = next_bank(Y_BANKS, "y", [P, CH], F32)
            nc.tensor.matmul(out=both[:], lhsT=ident_bf[:], rhs=p0[:, cols], start=True, stop=False)
            nc.tensor.matmul(out=both[:], lhsT=ident_bf[:], rhs=h0[:, cols], start=False, stop=True)
            o0 = o0_pool.tile([P, CH], F32, name="o0")
            nc.scalar.mul(out=o0[:], in_=both[:], mul=0.5)
            nc.sync.dma_start(out=out[0].rearrange("b c h w -> (b c) (h w)")[:, cols], in_=o0[:])

        def conv(m, c):
            y = next_bank(Y_BANKS, "y", [P, CH], F32)
            conv_pass(y[:], m, c, 0, CH, True, True)
            return y

        def add_to_sum(m, c):
            for q in range(CH // SUM_W):
                conv_pass(
                    acc[m][:],
                    m,
                    c,
                    q * SUM_W,
                    (q + 1) * SUM_W,
                    c == 0 and q == 0,
                    c == N_CH - 1 and q == CH // SUM_W - 1,
                )

        def square(y, m, c):
            junk = junk_pool.tile([P, CH], BF16, name="junk")
            nc.scalar.activation(
                out=junk[:],
                in_=y[:],
                func=ACT.Square,
                scale=N_PIX**-0.5,
                accum_out=ssq[:, m, c : c + 1] if c < N_CH - 1 else ssq_last[:, m : m + 1],
            )

        def load_node(k):
            m, rest = divmod(k, 2 * BATCH)
            b, j = divmod(rest, 2)
            nc.sync.dma_start(
                out=node_sb[j:P:2, m, b, :],
                in_=p_nodes[1 + 2 * m + j, b].rearrange("c h w -> c (h w)"),
            )

        par_mixed = const.tile([P, P], BF16)
        par = keep.tile([P, 2 * N_TILES], F32)
        sums = keep.tile([P, N_TILES], F32)
        mean_sq = keep.tile([P, N_TILES], F32)
        part_sq = keep.tile([P, N_TILES], F32)
        part_eps = keep.tile([P, N_TILES], F32)
        rest = keep.tile([P, N_TILES], F32)
        shift = keep.tile([P, N_TILES], F32)
        var_eps = keep.tile([P, N_TILES], F32)
        std = keep.tile([P, N_TILES], F32)
        rstd = keep.tile([P, N_TILES], F32)
        half_gain = keep.tile([P, N_TILES], F32)
        half_bias = keep.tile([P, N_TILES], F32)
        eps = const.tile([P, 1], F32)
        nc.vector.tensor_scalar(out=eps[:], in0=one[:], scalar1=EPS, scalar2=None, op0=ALU.mult)

        def total(m):
            nc.vector.tensor_reduce(out=sums[:, m : m + 1], in_=acc[m][:], axis=AX.X, op=ALU.add)

        def squares_so_far():
            nc.vector.tensor_reduce(out=part_sq[:], in_=ssq[:], axis=AX.X, op=ALU.add)

        def add_eps():
            nc.vector.tensor_scalar(out=part_eps[:], in0=part_sq[:], scalar1=EPS, scalar2=None, op0=ALU.add)

        def mean_square(m):
            nc.vector.scalar_tensor_tensor(
                out=mean_sq[:, m : m + 1],
                in0=sums[:, m : m + 1],
                scalar=1.0 / (N_PIX * N_PIX),
                in1=sums[:, m : m + 1],
                op0=ALU.mult,
                op1=ALU.mult,
            )

        def prepare(m):
            nc.vector.tensor_tensor(
                out=rest[:, m : m + 1], in0=part_eps[:, m : m + 1], in1=mean_sq[:, m : m + 1], op=ALU.subtract
            )
            nc.vector.scalar_tensor_tensor(
                out=shift[:, m : m + 1],
                in0=sums[:, m : m + 1],
                scalar=-1.0 / N_PIX,
                in1=par[:, m : m + 1],
                op0=ALU.mult,
                op1=ALU.mult,
            )

        def variance(m):
            nc.vector.tensor_scalar(
                out=var_eps[:, m : m + 1],
                in0=ssq_last[:, m : m + 1],
                scalar1=rest[:, m : m + 1],
                scalar2=eps[:],
                op0=ALU.add,
                op1=ALU.max,
            )

        def root(m):
            nc.scalar.activation(out=std[:, m : m + 1], in_=var_eps[:, m : m + 1], func=ACT.Sqrt)

        def reciprocal(m):
            nc.vector.reciprocal(out=rstd[:, m : m + 1], in_=std[:, m : m + 1])

        def gain_and_bias(m):
            nc.vector.tensor_tensor(
                out=half_gain[:, m : m + 1], in0=rstd[:, m : m + 1], in1=par[:, m : m + 1], op=ALU.mult
            )
            nc.vector.tensor_scalar(
                out=half_bias[:, m : m + 1],
                in0=rstd[:, m : m + 1],
                scalar1=shift[:, m : m + 1],
                scalar2=par[:, N_TILES + m : N_TILES + m + 1],
                op0=ALU.mult,
                op1=ALU.add,
            )

        small_steps = {
            0: (prepare, 1),
            1: (variance, 1),
            2: (total, 2),
            3: (root, 1),
            4: (reciprocal, 1),
            5: (gain_and_bias, 1),
            9: (mean_square, 2),
            10: (prepare, 2),
            11: (variance, 2),
            13: (root, 2),
            14: (reciprocal, 2),
            15: (gain_and_bias, 2),
        }

        banks = {}
        for step in range(N_CH + 3):
            if step == 3:
                nc.scalar.mul(out=par[:], in_=par_t[:, 0 : 2 * N_TILES], mul=0.5)
                for m in range(N_TILES):
                    acc_m = psum.tile([P, SUM_W], F32, tag="bank%d" % SUM_BANKS[m], name="acc%d" % m)
                    acc.append(acc_m)
            if step < N_CH:
                regroup(step)
            c = step - 1
            if c == N_CH - 1:
                quantise(c - 1)
            for lo in (0, HALF) if c == 0 else ():
                weigh(c, 0, banks[c, 0], lo, lo + HALF)
                weigh(c, 1, banks[c, 1], lo, lo + HALF)
            if 0 < c < N_CH:
                weigh(c, 0, banks[c, 0])
                weigh(c, 1, banks[c, 1])
            if c == N_CH - 1:
                quantise_branch(c, 0)
                quantise_branch(c, 1)
            c = step - 2
            if c == 0:
                quantise_weights()
            if 0 <= c < N_CH - 2:
                quantise(c)
            if step < N_CH:
                if step + RAW_SLOTS < N_CH:
                    load_chunk(step + RAW_SLOTS)
                if step == 1:
                    nc.sync.dma_start(out=p0[:], in_=p_nodes[0].rearrange("b c h w -> (b c) (h w)"))
                if step == 2:
                    nc.sync.dma_start(out=h0[:], in_=h_nodes[0].rearrange("b c h w -> (b c) (h w)"))
                if 3 <= step < N_TILES * BATCH * 2 + 3:
                    load_node(step - 3)
            c = step - 3
            if 0 <= c < N_CH - 1:
                ys = []
                for m in range(N_TILES):
                    ys.append(conv(m, c))
                for m in range(N_TILES):
                    add_to_sum(m, c)
                    square(ys[m], m, c)
            if c == N_CH - 1:
                for m in range(2):
                    add_to_sum(m, c)
                    y_last = conv(m, c)
                    if m == 1:
                        root(0)
                    square(y_last, m, c)
                    if m == 0:
                        total(0)
                        squares_so_far()
                        mean_square(0)
                        add_eps()
                        prepare(0)
                        variance(0)
                reciprocal(0)
                gain_and_bias(0)
                total(1)
                mean_square(1)
            if step == 0:
                banks[0, 0] = first_att[:]
            elif step < N_CH:
                banks[step, 0] = spread_attention(step, 0)
            if step in NODE0_STEPS:
                node0_bank(NODE0_STEPS.index(step))
            if step < N_CH:
                banks[step, 1] = spread_attention(step, 1)
            if step == 1:
                turn_weights()
            if step == 2:
                nc.scalar.copy(
                    out=par_mixed[:].rearrange("r (h j) -> r h j", j=2),
                    in_=par_rows[:].rearrange("r (j h) -> r h j", j=2),
                )
                nc.tensor.transpose(par_t[:], par_mixed[:], ident_bf[:])

        groups = []
        for m in range(N_TILES):
            for b in range(BATCH):
                sizes = (4, 4)
                if (m, b) == (0, 0):
                    sizes = (1, 1, 2, 4)
                if (m, b) == (N_TILES - 1, BATCH - 1):
                    sizes = (4, 2, 1, 1)
                k0 = 0
                for n in sizes:
                    groups.append((m, b, k0, n))
                    k0 += n
        n_added = 0
        for g, (m, b, k0, n) in enumerate(groups):
            r = g % N_REGIONS
            t = arena[:, r * REGION_EL : r * REGION_EL + 2 * n * CH].bitcast(F32)
            cols = slice(k0 * CH, (k0 + n) * CH)
            for k in range(n):
                z = next_bank(Z_BANKS, "z", [P, CH], F32)
                conv_pass(z[:], m, b * CH_PER_IMAGE + k0 + k, 0, CH, True, True)
                nc.scalar.activation(
                    out=t[:, k * CH : (k + 1) * CH],
                    in_=z[:],
                    func=ACT.Relu,
                    scale=half_gain[:, m : m + 1],
                    bias=half_bias[:, m : m + 1],
                )
                alone = g < 3 or g >= len(groups) - 3
                if alone or k % 2 == 1 or k == n - 1:
                    a = k - 1 if (k % 2 == 1 and not alone) else k
                    nc.vector.scalar_tensor_tensor(
                        out=t[:, a * CH : (k + 1) * CH],
                        in0=node_sb[:, m, b, (k0 + a) * CH : (k0 + k + 1) * CH],
                        scalar=0.5,
                        in1=t[:, a * CH : (k + 1) * CH],
                        op0=ALU.mult,
                        op1=ALU.add,
                    )
                    if n_added in small_steps:
                        step_of, tile = small_steps[n_added]
                        step_of(tile)
                    n_added += 1
            if g == 0:
                add_to_sum(2, N_CH - 1)
                y_last = conv(2, N_CH - 1)
                square(y_last, 2, N_CH - 1)
            for j in range(2):
                nc.sync.dma_start(
                    out=out[1 + 2 * m + j, b].rearrange("c h w -> c (h w)")[:, cols],
                    in_=t[j:P:2, :],
                )
